import numpy as np
import ml_dtypes


def mxq(x, axis, fmt="e4m3"):
    dtype, down = {"e4m3": (ml_dtypes.float8_e4m3fn, 7), "e5m2": (ml_dtypes.float8_e5m2, 14)}[fmt]
    v = np.moveaxis(np.asarray(x, np.float32).astype(ml_dtypes.bfloat16).astype(np.float64), axis, -1)
    blocks = v.reshape(v.shape[:-1] + (-1, 32))
    amax = np.abs(blocks).max(-1, keepdims=True)
    byte = np.maximum(np.where(amax > 0, np.frexp(amax)[1] - 1 + 127, 0) - down, 1)
    scale = np.exp2(byte - 127.0)
    codes = (blocks / scale).astype(np.float32).astype(dtype).astype(np.float64)
    return np.moveaxis((codes * scale).reshape(v.shape), -1, axis)


WIDE = False


def mx_kscale(k):
    if not WIDE:
        return np.ones(k)
    levels = np.array([20, -20, 10, -10, 0])
    a = np.random.permutation(np.resize(levels, k // 512 * 4)).reshape(k // 512, 4)
    idx = np.arange(k)
    return np.exp2(a[idx // 512, idx % 128 // 32])


BF16 = ml_dtypes.bfloat16


def bf(x):
    return np.asarray(x, np.float32).astype(BF16)


def f64(x):
    return np.asarray(x).astype(np.float64)


C, S, L, D, NK = 32, 1024, 3, 32, 48
COUNTS = [len(range(h, NK, L)) for h in range(L)]
K2 = COUNTS[1]


def conv_pre(E, W, b, h):
    P = L - h + 1
    k = W.shape[0]
    Et = np.transpose(E, (1, 0, 2, 3))
    win = np.stack([Et[:, :, p:p + h, :] for p in range(P)], axis=0).reshape(P * S, C * h * D)
    cv = (win @ W.reshape(k * C, C * h * D).T).reshape(P, S, k, C).transpose(0, 2, 1, 3)
    return cv + b[None, :, None, :]


def setup_inputs():
    s = mx_kscale(S)[None, :, None, None]
    Ec0 = bf(np.random.standard_normal((C, S, L, D)))
    inp = {'Ec': None}
    for h in range(1, L + 1):
        inp['W%d' % h] = bf(np.random.standard_normal((COUNTS[h - 1], C, C, h, D)) / np.sqrt(C * h * D))
    for h in range(1, L + 1):
        inp['b%d' % h] = bf(np.random.standard_normal((COUNTS[h - 1], C)) * 0.3)
    g = bf(np.random.standard_normal((C, S, 1, NK)) * np.exp2(np.random.randint(-12, 1, (1, S, 1, 1))) / s)
    cv = conv_pre(f64(Ec0), f64(inp['W2']), f64(inp['b2']), 2)
    inp['Ec'] = bf(f64(Ec0) * s)
    inp['conv2'] = np.asarray(cv, np.float32)
    inp['grad_out'] = g
    return inp


def reference(Ec, W1, W2, W3, b1, b2, b3, conv2, grad_out):
    cv = f64(conv2)
    g2 = np.transpose(f64(grad_out)[:, :, 0, 1::L], (2, 1, 0))
    live = (np.maximum(cv[0], cv[1]) > 0.0) * 1.0
    sel0 = (cv[0] > cv[1]) * 1.0 + (cv[0] == cv[1]) * 0.5
    sel = [sel0, 1.0 - sel0]
    Eq = mxq(np.transpose(f64(Ec), (1, 0, 2, 3)).reshape(S, C * L * D), 0, 'e4m3').reshape(S, C, L, D)
    total = 0.0
    for p in range(2):
        dconv = g2 * live * sel[p]
        gq = mxq(np.transpose(dconv, (1, 0, 2)).reshape(S, K2 * C), 0, 'e5m2')
        a = Eq[:, :, p:p + 2, :].reshape(S, C * 2 * D)
        total = total + (gq.T @ a)
    return total.reshape(K2, C, C, 2, D)

@@ -1,0 +1,161 @@
+import concourse.mybir as mybir
+
+F32 = mybir.dt.float32
+BF16 = mybir.dt.bfloat16
+U32 = mybir.dt.uint32
+U8 = mybir.dt.uint8
+E4M3_X4 = mybir.dt.float8_e4m3fn_x4
+E5M2_X4 = mybir.dt.float8_e5m2_x4
+ALU = mybir.AluOpType
+ACT = mybir.ActivationFunctionType
+
+C, S, L, D = 32, 1024, 3, 32
+HEIGHTS = 3
+K2 = 16
+POSITIONS = 2
+TAPS = 2
+
+P = 128
+PACK = 4
+PASSES = S // (P * PACK)
+
+M_TILE = P
+M_TILES = K2 * C // M_TILE
+C_GROUP = 8
+GROUPS = C // C_GROUP
+ROW_COLS = C_GROUP * D
+N_TILE = TAPS * ROW_COLS
+MASK_COLS = K2 * PACK * C
+
+FLOPS = 2 * POSITIONS * (K2 * C) * (C * TAPS * D) * S
+BYTES = 2 * C * S * L * D + 4 * POSITIONS * K2 * S * C + 2 * C * S * K2 + 4 * K2 * C * C * TAPS * D
+
+
+def quantise_dconv(nc, work, conv_raw, grad_raw, codes, scales):
+    conv_0 = conv_raw[:, 0:K2, :].rearrange("p j w -> p (j w)")
+    conv_1 = conv_raw[:, K2 : 2 * K2, :].rearrange("p j w -> p (j w)")
+
+    top = work.tile([P, MASK_COLS], F32)
+    nc.vector.scalar_tensor_tensor(out=top[:], in0=conv_0, scalar=0.0, in1=conv_1, op0=ALU.max, op1=ALU.max)
+    live = work.tile([P, MASK_COLS], BF16)
+    nc.scalar.activation(out=live[:], in_=top[:], func=ACT.Sign)
+
+    wins = work.tile([P, MASK_COLS], BF16)
+    nc.vector.tensor_tensor(out=wins[:], in0=conv_0, in1=conv_1, op=ALU.is_gt)
+    ties = work.tile([P, MASK_COLS], BF16)
+    nc.vector.tensor_tensor(out=ties[:], in0=conv_0, in1=conv_1, op=ALU.is_equal)
+    sel_0 = work.tile([P, MASK_COLS], BF16)
+    nc.vector.scalar_tensor_tensor(out=sel_0[:], in0=ties[:], scalar=0.5, in1=wins[:], op0=ALU.mult, op1=ALU.add)
+
+    mask_0 = work.tile([P, MASK_COLS], BF16)
+    nc.vector.tensor_tensor(out=mask_0[:], in0=live[:], in1=sel_0[:], op=ALU.mult)
+    mask_1 = work.tile([P, MASK_COLS], BF16)
+    nc.vector.tensor_tensor(out=mask_1[:], in0=live[:], in1=mask_0[:], op=ALU.subtract)
+
+    g2 = grad_raw[:].rearrange("p o (t j h) -> p h j o t", t=PACK, j=K2, h=HEIGHTS)[:, 1]
+    grouped = []
+    for position, mask in enumerate((mask_0, mask_1)):
+        dconv = work.tile([P, K2, C, PACK], BF16, align_bytes=64, name="dconv_%d" % position)
+        nc.vector.tensor_tensor(
+            out=dconv[:],
+            in0=mask[:].rearrange("p (j t o) -> p j o t", j=K2, t=PACK, o=C),
+            in1=g2,
+            op=ALU.mult,
+        )
+        grouped.append(dconv)
+    for position in range(POSITIONS):
+        nc.vector.quantize_mx(
+            out=codes[:, position, :].bitcast(E5M2_X4),
+            scales=scales[:, position, :],
+            in_=grouped[position][:].rearrange("p j o t -> p (j o t)"),
+        )
+
+
+def quantise_ec(nc, stage, ec_raw, codes, scales):
+    by_row = ec_raw[:].rearrange("p c (t l d) -> p l c d t", t=PACK, l=L, d=D)
+    grouped = []
+    for l in range(L):
+        ec_grouped = stage.tile([P, C_GROUP, D, PACK], BF16, align_bytes=64)
+        if l == 0:
+            nc.vector.tensor_copy(out=ec_grouped[:], in_=by_row[:, l])
+        else:
+            nc.scalar.copy(out=ec_grouped[:], in_=by_row[:, l])
+        grouped.append(ec_grouped)
+    for l in range(L):
+        row_cols = slice(l * ROW_COLS, (l + 1) * ROW_COLS)
+        nc.vector.quantize_mx(
+            out=codes[:, row_cols].bitcast(E4M3_X4),
+            scales=scales[:, row_cols],
+            in_=grouped[l][:].rearrange("p c d t -> p (c d t)"),
+        )
+
+
+def tile_vrtconv_v_kernel(tc, Ec, W1, W2, W3, b1, b2, b3, conv2, grad_out, out):
+    nc = tc.nc
+
+    conv_rows = conv2.rearrange("q j (g p t) o -> g p (q j) (t o)", g=PASSES, p=P, t=PACK)
+    grad_rows = grad_out.rearrange("o (g p t) x n -> g p o (t x n)", g=PASSES, p=P, t=PACK)
+    ec_rows = Ec.rearrange("c (g p t) l d -> g p c (t l d)", g=PASSES, p=P, t=PACK)
+    out_rows = out.rearrange("j o c a d -> (j o) (c a d)")
+
+    with tc.tile_pool(name="inputs", bufs=1) as inputs, tc.tile_pool(name="operands", bufs=1) as operands, tc.tile_pool(
+        name="work", bufs=1
+    ) as work, tc.tile_pool(name="stage", bufs=2 * L) as stage, tc.tile_pool(
+        name="results", bufs=M_TILES
+    ) as results, tc.psum_pool(name="psum", bufs=2) as psum:
+        conv_raw = []
+        grad_raw = []
+        for g in range(PASSES):
+            conv_raw.append(inputs.tile([P, POSITIONS * K2, PACK * C], F32, name="conv_raw_%d" % g))
+            nc.sync.dma_start(out=conv_raw[g][:], in_=conv_rows[g])
+        for g in range(PASSES):
+            grad_raw.append(inputs.tile([P, C, PACK * HEIGHTS * K2], BF16, name="grad_raw_%d" % g))
+            nc.sync.dma_start(out=grad_raw[g][:], in_=grad_rows[g])
+        ec_raw = {}
+        for group in range(GROUPS):
+            channels = slice(group * C_GROUP, (group + 1) * C_GROUP)
+            for g in range(PASSES):
+                ec_raw[group, g] = inputs.tile([P, C_GROUP, PACK * L * D], BF16, name="ec_raw_%d_%d" % (group, g))
+                nc.sync.dma_start(out=ec_raw[group, g][:], in_=ec_rows[g][:, channels, :])
+
+        dconv_codes = operands.tile([P, PASSES, POSITIONS, K2 * C], U32, align_bytes=64)
+        dconv_scales = operands.tile([P, PASSES, POSITIONS, K2 * C], U8, align_bytes=64)
+        ec_codes = operands.tile([P, PASSES, GROUPS, L * ROW_COLS], U32, align_bytes=64)
+        ec_scales = operands.tile([P, PASSES, GROUPS, L * ROW_COLS], U8, align_bytes=64)
+
+        for g in range(PASSES):
+            quantise_dconv(nc, work, conv_raw[g], grad_raw[g], dconv_codes[:, g], dconv_scales[:, g])
+
+        for group in range(GROUPS):
+            for g in range(PASSES):
+                quantise_ec(nc, stage, ec_raw[group, g], ec_codes[:, g, group, :], ec_scales[:, g, group, :])
+
+            sums = []
+            for m in range(M_TILES):
+                sums.append(psum.tile([M_TILE, N_TILE], F32, name="sums_%d" % m))
+            for g in range(PASSES):
+                for m in range(M_TILES):
+                    m_rows = slice(m * M_TILE, (m + 1) * M_TILE)
+                    for position in range(POSITIONS):
+                        window = slice(position * ROW_COLS, position * ROW_COLS + N_TILE)
+                        nc.tensor.matmul_mx(
+                            out=sums[m][:],
+                            lhsT=dconv_codes[:, g, position, m_rows].bitcast(E5M2_X4),
+                            lhsT_scale=dconv_scales[:, g, position, m_rows],
+                            rhs=ec_codes[:, g, group, window].bitcast(E4M3_X4),
+                            rhs_scale=ec_scales[:, g, group, window],
+                            start=(g == 0 and position == 0),
+                            stop=(g == PASSES - 1 and position == POSITIONS - 1),
+                        )
+
+            for m in range(M_TILES):
+                result = results.tile([M_TILE, C_GROUP, TAPS, D], F32)
+                in_order = sums[m][:].rearrange("p (a c d) -> p c a d", a=TAPS, c=C_GROUP, d=D)
+                if m % 2 == 0:
+                    nc.scalar.copy(out=result[:], in_=in_order)
+                else:
+                    nc.vector.tensor_copy(out=result[:], in_=in_order)
+                nc.sync.dma_start(
+                    out=out_rows[m * M_TILE : (m + 1) * M_TILE, group * N_TILE : (group + 1) * N_TILE],
+                    in_=result[:].rearrange("p c a d -> p (c a d)"),
+                )

@@ -7,7 +7,6 @@ U8 = mybir.dt.uint8
 E4M3_X4 = mybir.dt.float8_e4m3fn_x4
 E5M2_X4 = mybir.dt.float8_e5m2_x4
 ALU = mybir.AluOpType
-ACT = mybir.ActivationFunctionType
 
 C, S, L, D = 32, 1024, 3, 32
 HEIGHTS = 3
@@ -25,20 +24,21 @@ C_GROUP = 8
 GROUPS = C // C_GROUP
 ROW_COLS = C_GROUP * D
 N_TILE = TAPS * ROW_COLS
-MASK_COLS = K2 * PACK * C
+J_BLOCK = 8
+J_BLOCKS = K2 // J_BLOCK
+BLOCK_COLS = J_BLOCK * C
+MASK_COLS = J_BLOCK * PACK * C
 
 FLOPS = 2 * POSITIONS * (K2 * C) * (C * TAPS * D) * S
 BYTES = 2 * C * S * L * D + 4 * POSITIONS * K2 * S * C + 2 * C * S * K2 + 4 * K2 * C * C * TAPS * D
 
 
-def quantise_dconv(nc, work, conv_raw, grad_raw, codes, scales):
-    conv_0 = conv_raw[:, 0:K2, :].rearrange("p j w -> p (j w)")
-    conv_1 = conv_raw[:, K2 : 2 * K2, :].rearrange("p j w -> p (j w)")
+def quantise_dconv(nc, work, conv_raw, g2_rows, codes, scales):
+    conv_0 = conv_raw[:, 0].rearrange("p j w -> p (j w)")
+    conv_1 = conv_raw[:, 1].rearrange("p j w -> p (j w)")
 
-    top = work.tile([P, MASK_COLS], F32)
-    nc.vector.scalar_tensor_tensor(out=top[:], in0=conv_0, scalar=0.0, in1=conv_1, op0=ALU.max, op1=ALU.max)
-    live = work.tile([P, MASK_COLS], BF16)
-    nc.scalar.activation(out=live[:], in_=top[:], func=ACT.Sign)
+    g2 = work.tile([P, J_BLOCK, PACK, C], BF16)
+    nc.scalar.copy(out=g2[:], in_=g2_rows)
 
     wins = work.tile([P, MASK_COLS], BF16)
     nc.vector.tensor_tensor(out=wins[:], in0=conv_0, in1=conv_1, op=ALU.is_gt)
@@ -47,27 +47,24 @@ def quantise_dconv(nc, work, conv_raw, grad_raw, codes, scales):
     sel_0 = work.tile([P, MASK_COLS], BF16)
     nc.vector.scalar_tensor_tensor(out=sel_0[:], in0=ties[:], scalar=0.5, in1=wins[:], op0=ALU.mult, op1=ALU.add)
 
-    mask_0 = work.tile([P, MASK_COLS], BF16)
-    nc.vector.tensor_tensor(out=mask_0[:], in0=live[:], in1=sel_0[:], op=ALU.mult)
-    mask_1 = work.tile([P, MASK_COLS], BF16)
-    nc.vector.tensor_tensor(out=mask_1[:], in0=live[:], in1=mask_0[:], op=ALU.subtract)
+    top = work.tile([P, MASK_COLS], F32)
+    nc.vector.tensor_tensor(out=top[:], in0=conv_0, in1=conv_1, op=ALU.max)
+    g2_live = work.tile([P, MASK_COLS], BF16)
+    nc.vector.scalar_tensor_tensor(
+        out=g2_live[:], in0=top[:], scalar=0.0, in1=g2[:].rearrange("p j t o -> p (j t o)"), op0=ALU.is_gt, op1=ALU.mult
+    )
 
-    g2 = grad_raw[:].rearrange("p o (t j h) -> p h j o t", t=PACK, j=K2, h=HEIGHTS)[:, 1]
-    grouped = []
-    for position, mask in enumerate((mask_0, mask_1)):
-        dconv = work.tile([P, K2, C, PACK], BF16, align_bytes=64, name="dconv_%d" % position)
-        nc.vector.tensor_tensor(
-            out=dconv[:],
-            in0=mask[:].rearrange("p (j t o) -> p j o t", j=K2, t=PACK, o=C),
-            in1=g2,
-            op=ALU.mult,
-        )
-        grouped.append(dconv)
-    for position in range(POSITIONS):
+    g2_live_grouped = g2_live[:].rearrange("p (j t o) -> p j o t", j=J_BLOCK, t=PACK, o=C)
+    sel_0_grouped = sel_0[:].rearrange("p (j t o) -> p j o t", j=J_BLOCK, t=PACK, o=C)
+    dconv_0 = work.tile([P, J_BLOCK, C, PACK], BF16, align_bytes=64)
+    nc.vector.tensor_tensor(out=dconv_0[:], in0=g2_live_grouped, in1=sel_0_grouped, op=ALU.mult)
+    dconv_1 = work.tile([P, J_BLOCK, C, PACK], BF16, align_bytes=64)
+    nc.vector.tensor_tensor(out=dconv_1[:], in0=g2_live_grouped, in1=dconv_0[:], op=ALU.subtract)
+    for position, dconv in enumerate((dconv_0, dconv_1)):
         nc.vector.quantize_mx(
             out=codes[:, position, :].bitcast(E5M2_X4),
             scales=scales[:, position, :],
-            in_=grouped[position][:].rearrange("p j o t -> p (j o t)"),
+            in_=dconv[:].rearrange("p j o t -> p (j o t)"),
         )
 
 
@@ -99,15 +96,22 @@ def tile_vrtconv_v_kernel(tc, Ec, W1, W2, W3, b1, b2, b3, conv2, grad_out, out):
     out_rows = out.rearrange("j o c a d -> (j o) (c a d)")
 
     with tc.tile_pool(name="inputs", bufs=1) as inputs, tc.tile_pool(name="operands", bufs=1) as operands, tc.tile_pool(
-        name="work", bufs=1
+        name="work", bufs=2
     ) as work, tc.tile_pool(name="stage", bufs=2 * L) as stage, tc.tile_pool(
         name="results", bufs=M_TILES
     ) as results, tc.psum_pool(name="psum", bufs=2) as psum:
-        conv_raw = []
+        conv_raw = {}
         grad_raw = []
         for g in range(PASSES):
-            conv_raw.append(inputs.tile([P, POSITIONS * K2, PACK * C], F32, name="conv_raw_%d" % g))
-            nc.sync.dma_start(out=conv_raw[g][:], in_=conv_rows[g])
+            for block in range(J_BLOCKS):
+                conv_raw[g, block] = inputs.tile(
+                    [P, POSITIONS, J_BLOCK, PACK * C], F32, name="conv_raw_%d_%d" % (g, block)
+                )
+                for position in range(POSITIONS):
+                    first_j = position * K2 + block * J_BLOCK
+                    nc.sync.dma_start(
+                        out=conv_raw[g, block][:, position], in_=conv_rows[g][:, first_j : first_j + J_BLOCK, :]
+                    )
         for g in range(PASSES):
             grad_raw.append(inputs.tile([P, C, PACK * HEIGHTS * K2], BF16, name="grad_raw_%d" % g))
             nc.sync.dma_start(out=grad_raw[g][:], in_=grad_rows[g])
@@ -124,7 +128,18 @@ def tile_vrtconv_v_kernel(tc, Ec, W1, W2, W3, b1, b2, b3, conv2, grad_out, out):
         ec_scales = operands.tile([P, PASSES, GROUPS, L * ROW_COLS], U8, align_bytes=64)
 
         for g in range(PASSES):
-            quantise_dconv(nc, work, conv_raw[g], grad_raw[g], dconv_codes[:, g], dconv_scales[:, g])
+            g2_rows = grad_raw[g][:].rearrange("p o (t j h) -> p h j t o", t=PACK, j=K2, h=HEIGHTS)[:, 1]
+            for block in range(J_BLOCKS):
+                kernels = slice(block * J_BLOCK, (block + 1) * J_BLOCK)
+                block_cols = slice(block * BLOCK_COLS, (block + 1) * BLOCK_COLS)
+                quantise_dconv(
+                    nc,
+                    work,
+                    conv_raw[g, block],
+                    g2_rows[:, kernels],
+                    dconv_codes[:, g, :, block_cols],
+                    dconv_scales[:, g, :, block_cols],
+                )
 
         for group in range(GROUPS):
             for g in range(PASSES):

@@ -7,6 +7,7 @@ U8 = mybir.dt.uint8
 E4M3_X4 = mybir.dt.float8_e4m3fn_x4
 E5M2_X4 = mybir.dt.float8_e5m2_x4
 ALU = mybir.AluOpType
+ACT = mybir.ActivationFunctionType
 
 C, S, L, D = 32, 1024, 3, 32
 HEIGHTS = 3
@@ -33,12 +34,9 @@ FLOPS = 2 * POSITIONS * (K2 * C) * (C * TAPS * D) * S
 BYTES = 2 * C * S * L * D + 4 * POSITIONS * K2 * S * C + 2 * C * S * K2 + 4 * K2 * C * C * TAPS * D
 
 
-def quantise_dconv(nc, work, conv_raw, g2_rows, codes, scales):
+def make_masks(nc, work, keep, conv_raw, name):
     conv_0 = conv_raw[:, 0].rearrange("p j w -> p (j w)")
     conv_1 = conv_raw[:, 1].rearrange("p j w -> p (j w)")
-
-    g2 = work.tile([P, J_BLOCK, PACK, C], BF16)
-    nc.scalar.copy(out=g2[:], in_=g2_rows)
 
     wins = work.tile([P, MASK_COLS], BF16)
     nc.vector.tensor_tensor(out=wins[:], in0=conv_0, in1=conv_1, op=ALU.is_gt)
@@ -48,23 +46,36 @@ def quantise_dconv(nc, work, conv_raw, g2_rows, codes, scales):
     nc.vector.scalar_tensor_tensor(out=sel_0[:], in0=ties[:], scalar=0.5, in1=wins[:], op0=ALU.mult, op1=ALU.add)
 
     top = work.tile([P, MASK_COLS], F32)
-    nc.vector.tensor_tensor(out=top[:], in0=conv_0, in1=conv_1, op=ALU.max)
-    g2_live = work.tile([P, MASK_COLS], BF16)
-    nc.vector.scalar_tensor_tensor(
-        out=g2_live[:], in0=top[:], scalar=0.0, in1=g2[:].rearrange("p j t o -> p (j t o)"), op0=ALU.is_gt, op1=ALU.mult
-    )
+    nc.vector.scalar_tensor_tensor(out=top[:], in0=conv_0, scalar=0.0, in1=conv_1, op0=ALU.max, op1=ALU.max)
+    live = work.tile([P, MASK_COLS], BF16)
+    nc.scalar.activation(out=live[:], in_=top[:], func=ACT.Sign)
 
-    g2_live_grouped = g2_live[:].rearrange("p (j t o) -> p j o t", j=J_BLOCK, t=PACK, o=C)
-    sel_0_grouped = sel_0[:].rearrange("p (j t o) -> p j o t", j=J_BLOCK, t=PACK, o=C)
-    dconv_0 = work.tile([P, J_BLOCK, C, PACK], BF16, align_bytes=64)
-    nc.vector.tensor_tensor(out=dconv_0[:], in0=g2_live_grouped, in1=sel_0_grouped, op=ALU.mult)
-    dconv_1 = work.tile([P, J_BLOCK, C, PACK], BF16, align_bytes=64)
-    nc.vector.tensor_tensor(out=dconv_1[:], in0=g2_live_grouped, in1=dconv_0[:], op=ALU.subtract)
-    for position, dconv in enumerate((dconv_0, dconv_1)):
+    mask_0 = work.tile([P, MASK_COLS], BF16)
+    nc.vector.tensor_tensor(out=mask_0[:], in0=live[:], in1=sel_0[:], op=ALU.mult)
+    mask_1 = work.tile([P, MASK_COLS], BF16)
+    nc.vector.tensor_tensor(out=mask_1[:], in0=live[:], in1=mask_0[:], op=ALU.subtract)
+
+    grouped = []
+    for position, mask in enumerate((mask_0, mask_1)):
+        mask_grouped = keep.tile([P, J_BLOCK, C, PACK], BF16, name="mask_%d_%s" % (position, name))
+        nc.scalar.copy(out=mask_grouped[:], in_=mask[:].rearrange("p (j t o) -> p j o t", j=J_BLOCK, t=PACK, o=C))
+        grouped.append(mask_grouped)
+    return grouped
+
+
+def quantise_dconv(nc, work, mask_pair, g2_cols, codes, scales):
+    g2 = work.tile([P, J_BLOCK, C, PACK], BF16)
+    nc.scalar.copy(out=g2[:], in_=g2_cols)
+    products = []
+    for position in range(POSITIONS):
+        dconv = work.tile([P, J_BLOCK, C, PACK], BF16, align_bytes=64, name="dconv_%d" % position)
+        nc.vector.tensor_tensor(out=dconv[:], in0=mask_pair[position][:], in1=g2[:], op=ALU.mult)
+        products.append(dconv)
+    for position in range(POSITIONS):
         nc.vector.quantize_mx(
             out=codes[:, position, :].bitcast(E5M2_X4),
             scales=scales[:, position, :],
-            in_=dconv[:].rearrange("p j o t -> p (j o t)"),
+            in_=products[position][:].rearrange("p j o t -> p (j o t)"),
         )
 
 
@@ -73,7 +84,7 @@ def quantise_ec(nc, stage, ec_raw, codes, scales):
     grouped = []
     for l in range(L):
         ec_grouped = stage.tile([P, C_GROUP, D, PACK], BF16, align_bytes=64)
-        if l == 0:
+        if l < L - 1:
             nc.vector.tensor_copy(out=ec_grouped[:], in_=by_row[:, l])
         else:
             nc.scalar.copy(out=ec_grouped[:], in_=by_row[:, l])
@@ -127,16 +138,20 @@ def tile_vrtconv_v_kernel(tc, Ec, W1, W2, W3, b1, b2, b3, conv2, grad_out, out):
         ec_codes = operands.tile([P, PASSES, GROUPS, L * ROW_COLS], U32, align_bytes=64)
         ec_scales = operands.tile([P, PASSES, GROUPS, L * ROW_COLS], U8, align_bytes=64)
 
+        mask_pairs = {}
         for g in range(PASSES):
-            g2_rows = grad_raw[g][:].rearrange("p o (t j h) -> p h j t o", t=PACK, j=K2, h=HEIGHTS)[:, 1]
+            for block in range(J_BLOCKS):
+                mask_pairs[g, block] = make_masks(nc, work, operands, conv_raw[g, block], "%d_%d" % (g, block))
+        for g in range(PASSES):
+            g2_cols = grad_raw[g][:].rearrange("p o (t j h) -> p h j o t", t=PACK, j=K2, h=HEIGHTS)[:, 1]
             for block in range(J_BLOCKS):
                 kernels = slice(block * J_BLOCK, (block + 1) * J_BLOCK)
                 block_cols = slice(block * BLOCK_COLS, (block + 1) * BLOCK_COLS)
                 quantise_dconv(
                     nc,
                     work,
-                    conv_raw[g, block],
-                    g2_rows[:, kernels],
+                    mask_pairs[g, block],
+                    g2_cols[:, kernels],
                     dconv_codes[:, g, :, block_cols],
                     dconv_scales[:, g, :, block_cols],
                 )
@@ -165,11 +180,7 @@ def tile_vrtconv_v_kernel(tc, Ec, W1, W2, W3, b1, b2, b3, conv2, grad_out, out):
 
             for m in range(M_TILES):
                 result = results.tile([M_TILE, C_GROUP, TAPS, D], F32)
-                in_order = sums[m][:].rearrange("p (a c d) -> p c a d", a=TAPS, c=C_GROUP, d=D)
-                if m % 2 == 0:
-                    nc.scalar.copy(out=result[:], in_=in_order)
-                else:
-                    nc.vector.tensor_copy(out=result[:], in_=in_order)
+                nc.scalar.copy(out=result[:], in_=sums[m][:].rearrange("p (a c d) -> p c a d", a=TAPS, c=C_GROUP, d=D))
                 nc.sync.dma_start(
                     out=out_rows[m * M_TILE : (m + 1) * M_TILE, group * N_TILE : (group + 1) * N_TILE],
                     in_=result[:].rearrange("p c a d -> p (c a d)"),

@@ -34,9 +34,14 @@ FLOPS = 2 * POSITIONS * (K2 * C) * (C * TAPS * D) * S
 BYTES = 2 * C * S * L * D + 4 * POSITIONS * K2 * S * C + 2 * C * S * K2 + 4 * K2 * C * C * TAPS * D
 
 
-def make_masks(nc, work, keep, conv_raw, name):
+def compare(nc, work, conv_raw):
     conv_0 = conv_raw[:, 0].rearrange("p j w -> p (j w)")
     conv_1 = conv_raw[:, 1].rearrange("p j w -> p (j w)")
+
+    top = work.tile([P, MASK_COLS], F32)
+    nc.vector.scalar_tensor_tensor(out=top[:], in0=conv_0, scalar=0.0, in1=conv_1, op0=ALU.max, op1=ALU.max)
+    live = work.tile([P, MASK_COLS], BF16)
+    nc.scalar.activation(out=live[:], in_=top[:], func=ACT.Sign)
 
     wins = work.tile([P, MASK_COLS], BF16)
     nc.vector.tensor_tensor(out=wins[:], in0=conv_0, in1=conv_1, op=ALU.is_gt)
@@ -44,28 +49,30 @@ def make_masks(nc, work, keep, conv_raw, name):
     nc.vector.tensor_tensor(out=ties[:], in0=conv_0, in1=conv_1, op=ALU.is_equal)
     sel_0 = work.tile([P, MASK_COLS], BF16)
     nc.vector.scalar_tensor_tensor(out=sel_0[:], in0=ties[:], scalar=0.5, in1=wins[:], op0=ALU.mult, op1=ALU.add)
+    return sel_0, live
 
-    top = work.tile([P, MASK_COLS], F32)
-    nc.vector.scalar_tensor_tensor(out=top[:], in0=conv_0, scalar=0.0, in1=conv_1, op0=ALU.max, op1=ALU.max)
-    live = work.tile([P, MASK_COLS], BF16)
-    nc.scalar.activation(out=live[:], in_=top[:], func=ACT.Sign)
 
+def make_masks(nc, work, keep, sel_0, live, name):
     mask_0 = work.tile([P, MASK_COLS], BF16)
     nc.vector.tensor_tensor(out=mask_0[:], in0=live[:], in1=sel_0[:], op=ALU.mult)
     mask_1 = work.tile([P, MASK_COLS], BF16)
     nc.vector.tensor_tensor(out=mask_1[:], in0=live[:], in1=mask_0[:], op=ALU.subtract)
 
-    grouped = []
+    mask_pair = []
     for position, mask in enumerate((mask_0, mask_1)):
         mask_grouped = keep.tile([P, J_BLOCK, C, PACK], BF16, name="mask_%d_%s" % (position, name))
         nc.scalar.copy(out=mask_grouped[:], in_=mask[:].rearrange("p (j t o) -> p j o t", j=J_BLOCK, t=PACK, o=C))
-        grouped.append(mask_grouped)
-    return grouped
+        mask_pair.append(mask_grouped)
+    return mask_pair
 
 
-def quantise_dconv(nc, work, mask_pair, g2_cols, codes, scales):
+def copy_g2(nc, work, g2_cols):
     g2 = work.tile([P, J_BLOCK, C, PACK], BF16)
     nc.scalar.copy(out=g2[:], in_=g2_cols)
+    return g2
+
+
+def quantise_dconv(nc, work, mask_pair, g2, codes, scales):
     products = []
     for position in range(POSITIONS):
         dconv = work.tile([P, J_BLOCK, C, PACK], BF16, align_bytes=64, name="dconv_%d" % position)
@@ -106,23 +113,23 @@ def tile_vrtconv_v_kernel(tc, Ec, W1, W2, W3, b1, b2, b3, conv2, grad_out, out):
     ec_rows = Ec.rearrange("c (g p t) l d -> g p c (t l d)", g=PASSES, p=P, t=PACK)
     out_rows = out.rearrange("j o c a d -> (j o) (c a d)")
 
-    with tc.tile_pool(name="inputs", bufs=1) as inputs, tc.tile_pool(name="operands", bufs=1) as operands, tc.tile_pool(
-        name="work", bufs=2
-    ) as work, tc.tile_pool(name="stage", bufs=2 * L) as stage, tc.tile_pool(
+    with tc.manual_schedule(), tc.tile_pool(name="inputs", bufs=1) as inputs, tc.tile_pool(
+        name="operands", bufs=1
+    ) as operands, tc.tile_pool(name="work", bufs=2) as work, tc.tile_pool(name="stage", bufs=2 * L) as stage, tc.tile_pool(
         name="results", bufs=M_TILES
     ) as results, tc.psum_pool(name="psum", bufs=2) as psum:
-        conv_raw = {}
-        grad_raw = []
+        blocks = []
         for g in range(PASSES):
             for block in range(J_BLOCKS):
-                conv_raw[g, block] = inputs.tile(
-                    [P, POSITIONS, J_BLOCK, PACK * C], F32, name="conv_raw_%d_%d" % (g, block)
-                )
-                for position in range(POSITIONS):
-                    first_j = position * K2 + block * J_BLOCK
-                    nc.sync.dma_start(
-                        out=conv_raw[g, block][:, position], in_=conv_rows[g][:, first_j : first_j + J_BLOCK, :]
-                    )
+                blocks.append((g, block))
+        conv_raw = []
+        for g, block in blocks:
+            conv_block = inputs.tile([P, POSITIONS, J_BLOCK, PACK * C], F32, name="conv_raw_%d_%d" % (g, block))
+            for position in range(POSITIONS):
+                first_j = position * K2 + block * J_BLOCK
+                nc.sync.dma_start(out=conv_block[:, position], in_=conv_rows[g][:, first_j : first_j + J_BLOCK, :])
+            conv_raw.append(conv_block)
+        grad_raw = []
         for g in range(PASSES):
             grad_raw.append(inputs.tile([P, C, PACK * HEIGHTS * K2], BF16, name="grad_raw_%d" % g))
             nc.sync.dma_start(out=grad_raw[g][:], in_=grad_rows[g])
@@ -138,27 +145,41 @@ def tile_vrtconv_v_kernel(tc, Ec, W1, W2, W3, b1, b2, b3, conv2, grad_out, out):
         ec_codes = operands.tile([P, PASSES, GROUPS, L * ROW_COLS], U32, align_bytes=64)
         ec_scales = operands.tile([P, PASSES, GROUPS, L * ROW_COLS], U8, align_bytes=64)
 
-        mask_pairs = {}
-        for g in range(PASSES):
-            for block in range(J_BLOCKS):
-                mask_pairs[g, block] = make_masks(nc, work, operands, conv_raw[g, block], "%d_%d" % (g, block))
-        for g in range(PASSES):
-            g2_cols = grad_raw[g][:].rearrange("p o (t j h) -> p h j o t", t=PACK, j=K2, h=HEIGHTS)[:, 1]
-            for block in range(J_BLOCKS):
-                kernels = slice(block * J_BLOCK, (block + 1) * J_BLOCK)
+        compared = []
+        mask_pairs = []
+        for i in range(len(blocks) + 1):
+            if i < len(blocks):
+                compared.append(compare(nc, work, conv_raw[i]))
+            if i > 0:
+                sel_0, live = compared[i - 1]
+                mask_pairs.append(make_masks(nc, work, operands, sel_0, live, "%d_%d" % blocks[i - 1]))
+
+        g2_tiles = []
+        for i in range(len(blocks) + 1):
+            if i < len(blocks):
+                g, block = blocks[i]
+                g2_cols = grad_raw[g][:].rearrange("p o (t j h) -> p h j o t", t=PACK, j=K2, h=HEIGHTS)[:, 1]
+                g2_tiles.append(copy_g2(nc, work, g2_cols[:, block * J_BLOCK : (block + 1) * J_BLOCK]))
+            if i > 0:
+                g, block = blocks[i - 1]
                 block_cols = slice(block * BLOCK_COLS, (block + 1) * BLOCK_COLS)
                 quantise_dconv(
                     nc,
                     work,
-                    mask_pairs[g, block],
-                    g2_cols[:, kernels],
+                    mask_pairs[i - 1],
+                    g2_tiles[i - 1],
                     dconv_codes[:, g, :, block_cols],
                     dconv_scales[:, g, :, block_cols],
                 )
 
-        for group in range(GROUPS):
-            for g in range(PASSES):
-                quantise_ec(nc, stage, ec_raw[group, g], ec_codes[:, g, group, :], ec_scales[:, g, group, :])
+        for group in range(-1, GROUPS):
+            if group + 1 < GROUPS:
+                for g in range(PASSES):
+                    quantise_ec(
+                        nc, stage, ec_raw[group + 1, g], ec_codes[:, g, group + 1, :], ec_scales[:, g, group + 1, :]
+                    )
+            if group < 0:
+                continue
 
             sums = []
             for m in range(M_TILES):

@@ -28,51 +28,41 @@ N_TILE = TAPS * ROW_COLS
 J_BLOCK = 8
 J_BLOCKS = K2 // J_BLOCK
 BLOCK_COLS = J_BLOCK * C
+RUN = 4
 MASK_COLS = J_BLOCK * PACK * C
 
 FLOPS = 2 * POSITIONS * (K2 * C) * (C * TAPS * D) * S
 BYTES = 2 * C * S * L * D + 4 * POSITIONS * K2 * S * C + 2 * C * S * K2 + 4 * K2 * C * C * TAPS * D
 
 
-def compare(nc, work, conv_raw):
+def make_masks(nc, work, keep, conv_raw, name):
     conv_0 = conv_raw[:, 0].rearrange("p j w -> p (j w)")
     conv_1 = conv_raw[:, 1].rearrange("p j w -> p (j w)")
 
+    difference = work.tile([P, MASK_COLS], F32)
+    nc.vector.tensor_tensor(out=difference[:], in0=conv_0, in1=conv_1, op=ALU.subtract)
     top = work.tile([P, MASK_COLS], F32)
     nc.vector.scalar_tensor_tensor(out=top[:], in0=conv_0, scalar=0.0, in1=conv_1, op0=ALU.max, op1=ALU.max)
-    live = work.tile([P, MASK_COLS], BF16)
-    nc.scalar.activation(out=live[:], in_=top[:], func=ACT.Sign)
 
-    wins = work.tile([P, MASK_COLS], BF16)
-    nc.vector.tensor_tensor(out=wins[:], in0=conv_0, in1=conv_1, op=ALU.is_gt)
-    ties = work.tile([P, MASK_COLS], BF16)
-    nc.vector.tensor_tensor(out=ties[:], in0=conv_0, in1=conv_1, op=ALU.is_equal)
-    sel_0 = work.tile([P, MASK_COLS], BF16)
-    nc.vector.scalar_tensor_tensor(out=sel_0[:], in0=ties[:], scalar=0.5, in1=wins[:], op0=ALU.mult, op1=ALU.add)
-    return sel_0, live
+    lead = work.tile([P, J_BLOCK, C, PACK], BF16)
+    nc.scalar.activation(
+        out=lead[:], in_=difference[:].rearrange("p (j t o) -> p j o t", j=J_BLOCK, t=PACK, o=C), func=ACT.Sign
+    )
+    live = work.tile([P, J_BLOCK, C, PACK], BF16)
+    nc.scalar.activation(out=live[:], in_=top[:].rearrange("p (j t o) -> p j o t", j=J_BLOCK, t=PACK, o=C), func=ACT.Sign)
 
-
-def make_masks(nc, work, keep, sel_0, live, name):
-    mask_0 = work.tile([P, MASK_COLS], BF16)
+    sel_0 = work.tile([P, J_BLOCK, C, PACK], BF16)
+    nc.vector.tensor_scalar(out=sel_0[:], in0=lead[:], scalar1=0.5, scalar2=0.5, op0=ALU.mult, op1=ALU.add)
+    mask_0 = keep.tile([P, J_BLOCK, C, PACK], BF16, name="mask_0_%s" % name)
     nc.vector.tensor_tensor(out=mask_0[:], in0=live[:], in1=sel_0[:], op=ALU.mult)
-    mask_1 = work.tile([P, MASK_COLS], BF16)
+    mask_1 = keep.tile([P, J_BLOCK, C, PACK], BF16, name="mask_1_%s" % name)
     nc.vector.tensor_tensor(out=mask_1[:], in0=live[:], in1=mask_0[:], op=ALU.subtract)
-
-    mask_pair = []
-    for position, mask in enumerate((mask_0, mask_1)):
-        mask_grouped = keep.tile([P, J_BLOCK, C, PACK], BF16, name="mask_%d_%s" % (position, name))
-        nc.scalar.copy(out=mask_grouped[:], in_=mask[:].rearrange("p (j t o) -> p j o t", j=J_BLOCK, t=PACK, o=C))
-        mask_pair.append(mask_grouped)
-    return mask_pair
+    return mask_0, mask_1
 
 
-def copy_g2(nc, work, g2_cols):
+def quantise_dconv(nc, work, mask_pair, g2_cols, codes, scales):
     g2 = work.tile([P, J_BLOCK, C, PACK], BF16)
     nc.scalar.copy(out=g2[:], in_=g2_cols)
-    return g2
-
-
-def quantise_dconv(nc, work, mask_pair, g2, codes, scales):
     products = []
     for position in range(POSITIONS):
         dconv = work.tile([P, J_BLOCK, C, PACK], BF16, align_bytes=64, name="dconv_%d" % position)
@@ -92,7 +82,10 @@ def quantise_ec(nc, stage, ec_raw, codes, scales):
     for l in range(L):
         ec_grouped = stage.tile([P, C_GROUP, D, PACK], BF16, align_bytes=64)
         if l < L - 1:
-            nc.vector.tensor_copy(out=ec_grouped[:], in_=by_row[:, l])
+            nc.vector.tensor_copy(
+                out=ec_grouped[:].rearrange("p c (e i) t -> p c e t i", i=RUN),
+                in_=by_row[:, l].rearrange("p c (e i) t -> p c e t i", i=RUN),
+            )
         else:
             nc.scalar.copy(out=ec_grouped[:], in_=by_row[:, l])
         grouped.append(ec_grouped)
@@ -113,23 +106,23 @@ def tile_vrtconv_v_kernel(tc, Ec, W1, W2, W3, b1, b2, b3, conv2, grad_out, out):
     ec_rows = Ec.rearrange("c (g p t) l d -> g p c (t l d)", g=PASSES, p=P, t=PACK)
     out_rows = out.rearrange("j o c a d -> (j o) (c a d)")
 
-    with tc.manual_schedule(), tc.tile_pool(name="inputs", bufs=1) as inputs, tc.tile_pool(
-        name="operands", bufs=1
-    ) as operands, tc.tile_pool(name="work", bufs=2) as work, tc.tile_pool(name="stage", bufs=2 * L) as stage, tc.tile_pool(
+    with tc.tile_pool(name="inputs", bufs=1) as inputs, tc.tile_pool(name="operands", bufs=1) as operands, tc.tile_pool(
+        name="work", bufs=2
+    ) as work, tc.tile_pool(name="stage", bufs=2 * L) as stage, tc.tile_pool(
         name="results", bufs=M_TILES
     ) as results, tc.psum_pool(name="psum", bufs=2) as psum:
-        blocks = []
+        conv_raw = {}
+        grad_raw = []
         for g in range(PASSES):
             for block in range(J_BLOCKS):
-                blocks.append((g, block))
-        conv_raw = []
-        for g, block in blocks:
-            conv_block = inputs.tile([P, POSITIONS, J_BLOCK, PACK * C], F32, name="conv_raw_%d_%d" % (g, block))
-            for position in range(POSITIONS):
-                first_j = position * K2 + block * J_BLOCK
-                nc.sync.dma_start(out=conv_block[:, position], in_=conv_rows[g][:, first_j : first_j + J_BLOCK, :])
-            conv_raw.append(conv_block)
-        grad_raw = []
+                conv_raw[g, block] = inputs.tile(
+                    [P, POSITIONS, J_BLOCK, PACK * C], F32, name="conv_raw_%d_%d" % (g, block)
+                )
+                for position in range(POSITIONS):
+                    first_j = position * K2 + block * J_BLOCK
+                    nc.sync.dma_start(
+                        out=conv_raw[g, block][:, position], in_=conv_rows[g][:, first_j : first_j + J_BLOCK, :]
+                    )
         for g in range(PASSES):
             grad_raw.append(inputs.tile([P, C, PACK * HEIGHTS * K2], BF16, name="grad_raw_%d" % g))
             nc.sync.dma_start(out=grad_raw[g][:], in_=grad_rows[g])
@@ -145,50 +138,36 @@ def tile_vrtconv_v_kernel(tc, Ec, W1, W2, W3, b1, b2, b3, conv2, grad_out, out):
         ec_codes = operands.tile([P, PASSES, GROUPS, L * ROW_COLS], U32, align_bytes=64)
         ec_scales = operands.tile([P, PASSES, GROUPS, L * ROW_COLS], U8, align_bytes=64)
 
-        compared = []
-        mask_pairs = []
-        for i in range(len(blocks) + 1):
-            if i < len(blocks):
-                compared.append(compare(nc, work, conv_raw[i]))
-            if i > 0:
-                sel_0, live = compared[i - 1]
-                mask_pairs.append(make_masks(nc, work, operands, sel_0, live, "%d_%d" % blocks[i - 1]))
-
-        g2_tiles = []
-        for i in range(len(blocks) + 1):
-            if i < len(blocks):
-                g, block = blocks[i]
-                g2_cols = grad_raw[g][:].rearrange("p o (t j h) -> p h j o t", t=PACK, j=K2, h=HEIGHTS)[:, 1]
-                g2_tiles.append(copy_g2(nc, work, g2_cols[:, block * J_BLOCK : (block + 1) * J_BLOCK]))
-            if i > 0:
-                g, block = blocks[i - 1]
+        mask_pairs = {}
+        for g in range(PASSES):
+            for block in range(J_BLOCKS):
+                mask_pairs[g, block] = make_masks(nc, work, operands, conv_raw[g, block], "%d_%d" % (g, block))
+        for g in range(PASSES):
+            g2_cols = grad_raw[g][:].rearrange("p o (t j h) -> p h j o t", t=PACK, j=K2, h=HEIGHTS)[:, 1]
+            for block in range(J_BLOCKS):
+                kernels = slice(block * J_BLOCK, (block + 1) * J_BLOCK)
                 block_cols = slice(block * BLOCK_COLS, (block + 1) * BLOCK_COLS)
                 quantise_dconv(
                     nc,
                     work,
-                    mask_pairs[i - 1],
-                    g2_tiles[i - 1],
+                    mask_pairs[g, block],
+                    g2_cols[:, kernels],
                     dconv_codes[:, g, :, block_cols],
                     dconv_scales[:, g, :, block_cols],
                 )
 
-        for group in range(-1, GROUPS):
-            if group + 1 < GROUPS:
-                for g in range(PASSES):
-                    quantise_ec(
-                        nc, stage, ec_raw[group + 1, g], ec_codes[:, g, group + 1, :], ec_scales[:, g, group + 1, :]
-                    )
-            if group < 0:
-                continue
+        for group in range(GROUPS):
+            for g in range(PASSES):
+                quantise_ec(nc, stage, ec_raw[group, g], ec_codes[:, g, group, :], ec_scales[:, g, group, :])
 
             sums = []
             for m in range(M_TILES):
                 sums.append(psum.tile([M_TILE, N_TILE], F32, name="sums_%d" % m))
             for g in range(PASSES):
-                for m in range(M_TILES):
-                    m_rows = slice(m * M_TILE, (m + 1) * M_TILE)
-                    for position in range(POSITIONS):
-                        window = slice(position * ROW_COLS, position * ROW_COLS + N_TILE)
+                for position in range(POSITIONS):
+                    window = slice(position * ROW_COLS, position * ROW_COLS + N_TILE)
+                    for m in range(M_TILES):
+                        m_rows = slice(m * M_TILE, (m + 1) * M_TILE)
                         nc.tensor.matmul_mx(
                             out=sums[m][:],
                             lhsT=dconv_codes[:, g, position, m_rows].bitcast(E5M2_X4),
@@ -201,7 +180,11 @@ def tile_vrtconv_v_kernel(tc, Ec, W1, W2, W3, b1, b2, b3, conv2, grad_out, out):
 
             for m in range(M_TILES):
                 result = results.tile([M_TILE, C_GROUP, TAPS, D], F32)
-                nc.scalar.copy(out=result[:], in_=sums[m][:].rearrange("p (a c d) -> p c a d", a=TAPS, c=C_GROUP, d=D))
+                in_order = sums[m][:].rearrange("p (a c d) -> p c a d", a=TAPS, c=C_GROUP, d=D)
+                if m < M_TILES - 1:
+                    nc.scalar.copy(out=result[:], in_=in_order)
+                else:
+                    nc.vector.tensor_copy(out=result[:], in_=in_order)
                 nc.sync.dma_start(
                     out=out_rows[m * M_TILE : (m + 1) * M_TILE, group * N_TILE : (group + 1) * N_TILE],
                     in_=result[:].rearrange("p c a d -> p (c a d)"),

@@ -60,9 +60,9 @@ def make_masks(nc, work, keep, conv_raw, name):
     return mask_0, mask_1
 
 
-def quantise_dconv(nc, work, mask_pair, g2_cols, codes, scales):
+def quantise_dconv(nc, work, mask_pair, g2_cols, copy_g2, codes, scales):
     g2 = work.tile([P, J_BLOCK, C, PACK], BF16)
-    nc.scalar.copy(out=g2[:], in_=g2_cols)
+    copy_g2(out=g2[:], in_=g2_cols)
     products = []
     for position in range(POSITIONS):
         dconv = work.tile([P, J_BLOCK, C, PACK], BF16, align_bytes=64, name="dconv_%d" % position)
@@ -123,13 +123,13 @@ def tile_vrtconv_v_kernel(tc, Ec, W1, W2, W3, b1, b2, b3, conv2, grad_out, out):
                     nc.sync.dma_start(
                         out=conv_raw[g, block][:, position], in_=conv_rows[g][:, first_j : first_j + J_BLOCK, :]
                     )
-        for g in range(PASSES):
-            grad_raw.append(inputs.tile([P, C, PACK * HEIGHTS * K2], BF16, name="grad_raw_%d" % g))
-            nc.sync.dma_start(out=grad_raw[g][:], in_=grad_rows[g])
         ec_raw = {}
         for group in range(GROUPS):
             channels = slice(group * C_GROUP, (group + 1) * C_GROUP)
             for g in range(PASSES):
+                if group == 0:
+                    grad_raw.append(inputs.tile([P, C, PACK * HEIGHTS * K2], BF16, name="grad_raw_%d" % g))
+                    nc.sync.dma_start(out=grad_raw[g][:], in_=grad_rows[g])
                 ec_raw[group, g] = inputs.tile([P, C_GROUP, PACK * L * D], BF16, name="ec_raw_%d_%d" % (group, g))
                 nc.sync.dma_start(out=ec_raw[group, g][:], in_=ec_rows[g][:, channels, :])
 
@@ -152,6 +152,7 @@ def tile_vrtconv_v_kernel(tc, Ec, W1, W2, W3, b1, b2, b3, conv2, grad_out, out):
                     work,
                     mask_pairs[g, block],
                     g2_cols[:, kernels],
+                    nc.scalar.copy if block % 2 == 0 else nc.vector.tensor_copy,
                     dconv_codes[:, g, :, block_cols],
                     dconv_scales[:, g, :, block_cols],
                 )
@@ -180,11 +181,7 @@ def tile_vrtconv_v_kernel(tc, Ec, W1, W2, W3, b1, b2, b3, conv2, grad_out, out):
 
             for m in range(M_TILES):
                 result = results.tile([M_TILE, C_GROUP, TAPS, D], F32)
-                in_order = sums[m][:].rearrange("p (a c d) -> p c a d", a=TAPS, c=C_GROUP, d=D)
-                if m < M_TILES - 1:
-                    nc.scalar.copy(out=result[:], in_=in_order)
-                else:
-                    nc.vector.tensor_copy(out=result[:], in_=in_order)
+                nc.scalar.copy(out=result[:], in_=sums[m][:].rearrange("p (a c d) -> p c a d", a=TAPS, c=C_GROUP, d=D))
                 nc.sync.dma_start(
                     out=out_rows[m * M_TILE : (m + 1) * M_TILE, group * N_TILE : (group + 1) * N_TILE],
                     in_=result[:].rearrange("p c a d -> p (c a d)"),

@@ -181,7 +181,11 @@ def tile_vrtconv_v_kernel(tc, Ec, W1, W2, W3, b1, b2, b3, conv2, grad_out, out):
 
             for m in range(M_TILES):
                 result = results.tile([M_TILE, C_GROUP, TAPS, D], F32)
-                nc.scalar.copy(out=result[:], in_=sums[m][:].rearrange("p (a c d) -> p c a d", a=TAPS, c=C_GROUP, d=D))
+                in_order = sums[m][:].rearrange("p (a c d) -> p c a d", a=TAPS, c=C_GROUP, d=D)
+                if group == GROUPS - 1 and m % 2 == 1:
+                    nc.vector.tensor_copy(out=result[:], in_=in_order)
+                else:
+                    nc.scalar.copy(out=result[:], in_=in_order)
                 nc.sync.dma_start(
                     out=out_rows[m * M_TILE : (m + 1) * M_TILE, group * N_TILE : (group + 1) * N_TILE],
                     in_=result[:].rearrange("p c a d -> p (c a d)"),

@@ -165,10 +165,10 @@ def tile_vrtconv_v_kernel(tc, Ec, W1, W2, W3, b1, b2, b3, conv2, grad_out, out):
             for m in range(M_TILES):
                 sums.append(psum.tile([M_TILE, N_TILE], F32, name="sums_%d" % m))
             for g in range(PASSES):
-                for position in range(POSITIONS):
-                    window = slice(position * ROW_COLS, position * ROW_COLS + N_TILE)
-                    for m in range(M_TILES):
-                        m_rows = slice(m * M_TILE, (m + 1) * M_TILE)
+                for m in range(M_TILES):
+                    m_rows = slice(m * M_TILE, (m + 1) * M_TILE)
+                    for position in range(POSITIONS):
+                        window = slice(position * ROW_COLS, position * ROW_COLS + N_TILE)
                         nc.tensor.matmul_mx(
                             out=sums[m][:],
                             lhsT=dconv_codes[:, g, position, m_rows].bitcast(E5M2_X4),
@@ -181,11 +181,7 @@ def tile_vrtconv_v_kernel(tc, Ec, W1, W2, W3, b1, b2, b3, conv2, grad_out, out):
 
             for m in range(M_TILES):
                 result = results.tile([M_TILE, C_GROUP, TAPS, D], F32)
-                in_order = sums[m][:].rearrange("p (a c d) -> p c a d", a=TAPS, c=C_GROUP, d=D)
-                if group == GROUPS - 1 and m % 2 == 1:
-                    nc.vector.tensor_copy(out=result[:], in_=in_order)
-                else:
-                    nc.scalar.copy(out=result[:], in_=in_order)
+                nc.scalar.copy(out=result[:], in_=sums[m][:].rearrange("p (a c d) -> p c a d", a=TAPS, c=C_GROUP, d=D))
                 nc.sync.dma_start(
                     out=out_rows[m * M_TILE : (m + 1) * M_TILE, group * N_TILE : (group + 1) * N_TILE],
                     in_=result[:].rearrange("p c a d -> p (c a d)"),

@@ -35,29 +35,27 @@ FLOPS = 2 * POSITIONS * (K2 * C) * (C * TAPS * D) * S
 BYTES = 2 * C * S * L * D + 4 * POSITIONS * K2 * S * C + 2 * C * S * K2 + 4 * K2 * C * C * TAPS * D
 
 
-def make_masks(nc, work, keep, conv_raw, name):
+def make_masks(nc, work, conv_raw, mask_0, mask_1):
+    kernels = conv_raw.shape[2]
     conv_0 = conv_raw[:, 0].rearrange("p j w -> p (j w)")
     conv_1 = conv_raw[:, 1].rearrange("p j w -> p (j w)")
 
-    difference = work.tile([P, MASK_COLS], F32)
+    difference = work.tile([P, kernels * PACK * C], F32)
     nc.vector.tensor_tensor(out=difference[:], in0=conv_0, in1=conv_1, op=ALU.subtract)
-    top = work.tile([P, MASK_COLS], F32)
+    top = work.tile([P, kernels * PACK * C], F32)
     nc.vector.scalar_tensor_tensor(out=top[:], in0=conv_0, scalar=0.0, in1=conv_1, op0=ALU.max, op1=ALU.max)
 
-    lead = work.tile([P, J_BLOCK, C, PACK], BF16)
+    lead = work.tile([P, kernels, C, PACK], BF16)
     nc.scalar.activation(
-        out=lead[:], in_=difference[:].rearrange("p (j t o) -> p j o t", j=J_BLOCK, t=PACK, o=C), func=ACT.Sign
+        out=lead[:], in_=difference[:].rearrange("p (j t o) -> p j o t", j=kernels, t=PACK, o=C), func=ACT.Sign
     )
-    live = work.tile([P, J_BLOCK, C, PACK], BF16)
-    nc.scalar.activation(out=live[:], in_=top[:].rearrange("p (j t o) -> p j o t", j=J_BLOCK, t=PACK, o=C), func=ACT.Sign)
+    live = work.tile([P, kernels, C, PACK], BF16)
+    nc.scalar.activation(out=live[:], in_=top[:].rearrange("p (j t o) -> p j o t", j=kernels, t=PACK, o=C), func=ACT.Sign)
 
-    sel_0 = work.tile([P, J_BLOCK, C, PACK], BF16)
+    sel_0 = work.tile([P, kernels, C, PACK], BF16)
     nc.vector.tensor_scalar(out=sel_0[:], in0=lead[:], scalar1=0.5, scalar2=0.5, op0=ALU.mult, op1=ALU.add)
-    mask_0 = keep.tile([P, J_BLOCK, C, PACK], BF16, name="mask_0_%s" % name)
-    nc.vector.tensor_tensor(out=mask_0[:], in0=live[:], in1=sel_0[:], op=ALU.mult)
-    mask_1 = keep.tile([P, J_BLOCK, C, PACK], BF16, name="mask_1_%s" % name)
-    nc.vector.tensor_tensor(out=mask_1[:], in0=live[:], in1=mask_0[:], op=ALU.subtract)
-    return mask_0, mask_1
+    nc.vector.tensor_tensor(out=mask_0, in0=live[:], in1=sel_0[:], op=ALU.mult)
+    nc.vector.tensor_tensor(out=mask_1, in0=live[:], in1=mask_0, op=ALU.subtract)
 
 
 def quantise_dconv(nc, work, mask_pair, g2_cols, copy_g2, codes, scales):
@@ -76,12 +74,12 @@ def quantise_dconv(nc, work, mask_pair, g2_cols, copy_g2, codes, scales):
         )
 
 
-def quantise_ec(nc, stage, ec_raw, codes, scales):
+def quantise_ec(nc, stage, ec_raw, vector_rows, codes, scales):
     by_row = ec_raw[:].rearrange("p c (t l d) -> p l c d t", t=PACK, l=L, d=D)
     grouped = []
     for l in range(L):
         ec_grouped = stage.tile([P, C_GROUP, D, PACK], BF16, align_bytes=64)
-        if l < L - 1:
+        if l < vector_rows:
             nc.vector.tensor_copy(
                 out=ec_grouped[:].rearrange("p c (e i) t -> p c e t i", i=RUN),
                 in_=by_row[:, l].rearrange("p c (e i) t -> p c e t i", i=RUN),
@@ -112,37 +110,61 @@ def tile_vrtconv_v_kernel(tc, Ec, W1, W2, W3, b1, b2, b3, conv2, grad_out, out):
         name="results", bufs=M_TILES
     ) as results, tc.psum_pool(name="psum", bufs=2) as psum:
         conv_raw = {}
-        grad_raw = []
-        for g in range(PASSES):
+        grad_raw = {}
+        ec_raw = {}
+
+        def pieces_of(g, block):
+            return 2 if g == 0 and block == 0 else 1
+
+        def load_conv(g):
             for block in range(J_BLOCKS):
                 conv_raw[g, block] = inputs.tile(
                     [P, POSITIONS, J_BLOCK, PACK * C], F32, name="conv_raw_%d_%d" % (g, block)
                 )
-                for position in range(POSITIONS):
-                    first_j = position * K2 + block * J_BLOCK
-                    nc.sync.dma_start(
-                        out=conv_raw[g, block][:, position], in_=conv_rows[g][:, first_j : first_j + J_BLOCK, :]
-                    )
-        ec_raw = {}
-        for group in range(GROUPS):
-            channels = slice(group * C_GROUP, (group + 1) * C_GROUP)
+                step = J_BLOCK // pieces_of(g, block)
+                for j in range(0, J_BLOCK, step):
+                    for position in range(POSITIONS):
+                        first_j = position * K2 + block * J_BLOCK + j
+                        nc.sync.dma_start(
+                            out=conv_raw[g, block][:, position, j : j + step],
+                            in_=conv_rows[g][:, first_j : first_j + step, :],
+                        )
+
+        def load_grad(g):
+            grad_raw[g] = inputs.tile([P, C, PACK * HEIGHTS * K2], BF16, name="grad_raw_%d" % g)
+            nc.sync.dma_start(out=grad_raw[g][:], in_=grad_rows[g])
+
+        def load_ec(group, g):
+            ec_raw[group, g] = inputs.tile([P, C_GROUP, PACK * L * D], BF16, name="ec_raw_%d_%d" % (group, g))
+            nc.sync.dma_start(out=ec_raw[group, g][:], in_=ec_rows[g][:, group * C_GROUP : (group + 1) * C_GROUP, :])
+
+        load_conv(0)
+        load_conv(1)
+        for g in range(PASSES):
+            load_grad(g)
+            load_ec(0, g)
+        for group in range(1, GROUPS):
             for g in range(PASSES):
-                if group == 0:
-                    grad_raw.append(inputs.tile([P, C, PACK * HEIGHTS * K2], BF16, name="grad_raw_%d" % g))
-                    nc.sync.dma_start(out=grad_raw[g][:], in_=grad_rows[g])
-                ec_raw[group, g] = inputs.tile([P, C_GROUP, PACK * L * D], BF16, name="ec_raw_%d_%d" % (group, g))
-                nc.sync.dma_start(out=ec_raw[group, g][:], in_=ec_rows[g][:, channels, :])
+                load_ec(group, g)
 
         dconv_codes = operands.tile([P, PASSES, POSITIONS, K2 * C], U32, align_bytes=64)
         dconv_scales = operands.tile([P, PASSES, POSITIONS, K2 * C], U8, align_bytes=64)
         ec_codes = operands.tile([P, PASSES, GROUPS, L * ROW_COLS], U32, align_bytes=64)
         ec_scales = operands.tile([P, PASSES, GROUPS, L * ROW_COLS], U8, align_bytes=64)
-
         mask_pairs = {}
-        for g in range(PASSES):
+
+        def masks_of(g):
             for block in range(J_BLOCKS):
-                mask_pairs[g, block] = make_masks(nc, work, operands, conv_raw[g, block], "%d_%d" % (g, block))
-        for g in range(PASSES):
+                mask_0 = operands.tile([P, J_BLOCK, C, PACK], BF16, name="mask_0_%d_%d" % (g, block))
+                mask_1 = operands.tile([P, J_BLOCK, C, PACK], BF16, name="mask_1_%d_%d" % (g, block))
+                mask_pairs[g, block] = (mask_0, mask_1)
+                step = J_BLOCK // pieces_of(g, block)
+                for j in range(0, J_BLOCK, step):
+                    make_masks(
+                        nc, work, conv_raw[g, block][:, :, j : j + step], mask_0[:, j : j + step], mask_1[:, j : j + step]
+                    )
+
+        def dconv_of(g):
             g2_cols = grad_raw[g][:].rearrange("p o (t j h) -> p h j o t", t=PACK, j=K2, h=HEIGHTS)[:, 1]
             for block in range(J_BLOCKS):
                 kernels = slice(block * J_BLOCK, (block + 1) * J_BLOCK)
@@ -157,10 +179,10 @@ def tile_vrtconv_v_kernel(tc, Ec, W1, W2, W3, b1, b2, b3, conv2, grad_out, out):
                     dconv_scales[:, g, :, block_cols],
                 )
 
-        for group in range(GROUPS):
-            for g in range(PASSES):
-                quantise_ec(nc, stage, ec_raw[group, g], ec_codes[:, g, group, :], ec_scales[:, g, group, :])
+        def ec_of(group, g, vector_rows):
+            quantise_ec(nc, stage, ec_raw[group, g], vector_rows, ec_codes[:, g, group, :], ec_scales[:, g, group, :])
 
+        def products_of(group):
             sums = []
             for m in range(M_TILES):
                 sums.append(psum.tile([M_TILE, N_TILE], F32, name="sums_%d" % m))
@@ -178,7 +200,6 @@ def tile_vrtconv_v_kernel(tc, Ec, W1, W2, W3, b1, b2, b3, conv2, grad_out, out):
                             start=(g == 0 and position == 0),
                             stop=(g == PASSES - 1 and position == POSITIONS - 1),
                         )
-
             for m in range(M_TILES):
                 result = results.tile([M_TILE, C_GROUP, TAPS, D], F32)
                 nc.scalar.copy(out=result[:], in_=sums[m][:].rearrange("p (a c d) -> p c a d", a=TAPS, c=C_GROUP, d=D))
@@ -186,3 +207,12 @@ def tile_vrtconv_v_kernel(tc, Ec, W1, W2, W3, b1, b2, b3, conv2, grad_out, out):
                     out=out_rows[m * M_TILE : (m + 1) * M_TILE, group * N_TILE : (group + 1) * N_TILE],
                     in_=result[:].rearrange("p c a d -> p (c a d)"),
                 )
+
+        for g in range(PASSES):
+            masks_of(g)
+        for g in range(PASSES):
+            dconv_of(g)
+        for group in range(GROUPS):
+            for g in range(PASSES):
+                ec_of(group, g, 1 if group == 0 else L - 1)
+            products_of(group)

@@ -28,34 +28,40 @@ N_TILE = TAPS * ROW_COLS
 J_BLOCK = 8
 J_BLOCKS = K2 // J_BLOCK
 BLOCK_COLS = J_BLOCK * C
+LEAST = 2.0**-126
 RUN = 4
-MASK_COLS = J_BLOCK * PACK * C
 
 FLOPS = 2 * POSITIONS * (K2 * C) * (C * TAPS * D) * S
 BYTES = 2 * C * S * L * D + 4 * POSITIONS * K2 * S * C + 2 * C * S * K2 + 4 * K2 * C * C * TAPS * D
 
 
-def make_masks(nc, work, conv_raw, mask_0, mask_1):
+def make_masks(nc, work, conv_raw, mask_pair):
     kernels = conv_raw.shape[2]
-    conv_0 = conv_raw[:, 0].rearrange("p j w -> p (j w)")
-    conv_1 = conv_raw[:, 1].rearrange("p j w -> p (j w)")
-
-    difference = work.tile([P, kernels * PACK * C], F32)
-    nc.vector.tensor_tensor(out=difference[:], in0=conv_0, in1=conv_1, op=ALU.subtract)
-    top = work.tile([P, kernels * PACK * C], F32)
-    nc.vector.scalar_tensor_tensor(out=top[:], in0=conv_0, scalar=0.0, in1=conv_1, op0=ALU.max, op1=ALU.max)
-
-    lead = work.tile([P, kernels, C, PACK], BF16)
+    conv = conv_raw.rearrange("p q j w -> p q (j w)")
+    behind = work.tile([P, POSITIONS, kernels * PACK * C], BF16)
+    for position in range(POSITIONS):
+        nc.vector.scalar_tensor_tensor(
+            out=behind[:, position],
+            in0=conv[:, 1 - position],
+            scalar=LEAST,
+            in1=conv[:, position],
+            op0=ALU.max,
+            op1=ALU.subtract,
+        )
+    side = work.tile([P, POSITIONS * kernels, C, PACK], BF16)
     nc.scalar.activation(
-        out=lead[:], in_=difference[:].rearrange("p (j t o) -> p j o t", j=kernels, t=PACK, o=C), func=ACT.Sign
+        out=side[:],
+        in_=behind[:].rearrange("p q (j t o) -> p (q j) o t", j=kernels, t=PACK, o=C),
+        func=ACT.Sign,
     )
-    live = work.tile([P, kernels, C, PACK], BF16)
-    nc.scalar.activation(out=live[:], in_=top[:].rearrange("p (j t o) -> p j o t", j=kernels, t=PACK, o=C), func=ACT.Sign)
-
-    sel_0 = work.tile([P, kernels, C, PACK], BF16)
-    nc.vector.tensor_scalar(out=sel_0[:], in0=lead[:], scalar1=0.5, scalar2=0.5, op0=ALU.mult, op1=ALU.add)
-    nc.vector.tensor_tensor(out=mask_0, in0=live[:], in1=sel_0[:], op=ALU.mult)
-    nc.vector.tensor_tensor(out=mask_1, in0=live[:], in1=mask_0, op=ALU.subtract)
+    nc.vector.tensor_scalar(
+        out=mask_pair,
+        in0=side[:].rearrange("p (q j) o t -> p q j o t", q=POSITIONS),
+        scalar1=-0.5,
+        scalar2=0.5,
+        op0=ALU.mult,
+        op1=ALU.add,
+    )
 
 
 def quantise_dconv(nc, work, mask_pair, g2_cols, copy_g2, codes, scales):
@@ -64,7 +70,7 @@ def quantise_dconv(nc, work, mask_pair, g2_cols, copy_g2, codes, scales):
     products = []
     for position in range(POSITIONS):
         dconv = work.tile([P, J_BLOCK, C, PACK], BF16, align_bytes=64, name="dconv_%d" % position)
-        nc.vector.tensor_tensor(out=dconv[:], in0=mask_pair[position][:], in1=g2[:], op=ALU.mult)
+        nc.vector.tensor_tensor(out=dconv[:], in0=mask_pair[:, position], in1=g2[:], op=ALU.mult)
         products.append(dconv)
     for position in range(POSITIONS):
         nc.vector.quantize_mx(
@@ -155,14 +161,11 @@ def tile_vrtconv_v_kernel(tc, Ec, W1, W2, W3, b1, b2, b3, conv2, grad_out, out):
 
         def masks_of(g):
             for block in range(J_BLOCKS):
-                mask_0 = operands.tile([P, J_BLOCK, C, PACK], BF16, name="mask_0_%d_%d" % (g, block))
-                mask_1 = operands.tile([P, J_BLOCK, C, PACK], BF16, name="mask_1_%d_%d" % (g, block))
-                mask_pairs[g, block] = (mask_0, mask_1)
+                mask_pair = operands.tile([P, POSITIONS, J_BLOCK, C, PACK], BF16, name="mask_pair_%d_%d" % (g, block))
+                mask_pairs[g, block] = mask_pair
                 step = J_BLOCK // pieces_of(g, block)
                 for j in range(0, J_BLOCK, step):
-                    make_masks(
-                        nc, work, conv_raw[g, block][:, :, j : j + step], mask_0[:, j : j + step], mask_1[:, j : j + step]
-                    )
+                    make_masks(nc, work, conv_raw[g, block][:, :, j : j + step], mask_pair[:, :, j : j + step])
 
         def dconv_of(g):
             g2_cols = grad_raw[g][:].rearrange("p o (t j h) -> p h j o t", t=PACK, j=K2, h=HEIGHTS)[:, 1]

@@ -27,7 +27,7 @@ ROW_COLS = C_GROUP * D
 N_TILE = TAPS * ROW_COLS
 J_BLOCK = 8
 J_BLOCKS = K2 // J_BLOCK
-BLOCK_COLS = J_BLOCK * C
+J_TILE = M_TILE // C
 LEAST = 2.0**-126
 RUN = 4
 
@@ -64,20 +64,15 @@ def make_masks(nc, work, conv_raw, mask_pair):
     )
 
 
-def quantise_dconv(nc, work, mask_pair, g2_cols, copy_g2, codes, scales):
-    g2 = work.tile([P, J_BLOCK, C, PACK], BF16)
+def multiply_dconv(nc, work, tile_masks, g2_cols, copy_g2):
+    g2 = work.tile([P, J_TILE, C, PACK], BF16)
     copy_g2(out=g2[:], in_=g2_cols)
-    products = []
+    dconv = work.tile([P, POSITIONS, M_TILE * PACK], BF16, align_bytes=64)
     for position in range(POSITIONS):
-        dconv = work.tile([P, J_BLOCK, C, PACK], BF16, align_bytes=64, name="dconv_%d" % position)
-        nc.vector.tensor_tensor(out=dconv[:], in0=mask_pair[:, position], in1=g2[:], op=ALU.mult)
-        products.append(dconv)
-    for position in range(POSITIONS):
-        nc.vector.quantize_mx(
-            out=codes[:, position, :].bitcast(E5M2_X4),
-            scales=scales[:, position, :],
-            in_=products[position][:].rearrange("p j o t -> p (j o t)"),
+        nc.vector.tensor_tensor(
+            out=dconv[:, position], in0=tile_masks[:, position], in1=g2[:].rearrange("p j o t -> p (j o t)"), op=ALU.mult
         )
+    return dconv
 
 
 def quantise_ec(nc, stage, ec_raw, vector_rows, codes, scales):
@@ -111,7 +106,7 @@ def tile_vrtconv_v_kernel(tc, Ec, W1, W2, W3, b1, b2, b3, conv2, grad_out, out):
     out_rows = out.rearrange("j o c a d -> (j o) (c a d)")
 
     with tc.tile_pool(name="inputs", bufs=1) as inputs, tc.tile_pool(name="operands", bufs=1) as operands, tc.tile_pool(
-        name="work", bufs=2
+        name="work", bufs=3
     ) as work, tc.tile_pool(name="stage", bufs=2 * L) as stage, tc.tile_pool(
         name="results", bufs=M_TILES
     ) as results, tc.psum_pool(name="psum", bufs=2) as psum:
@@ -153,8 +148,8 @@ def tile_vrtconv_v_kernel(tc, Ec, W1, W2, W3, b1, b2, b3, conv2, grad_out, out):
             for g in range(PASSES):
                 load_ec(group, g)
 
-        dconv_codes = operands.tile([P, PASSES, POSITIONS, K2 * C], U32, align_bytes=64)
-        dconv_scales = operands.tile([P, PASSES, POSITIONS, K2 * C], U8, align_bytes=64)
+        dconv_codes = operands.tile([P, PASSES, M_TILES, POSITIONS, M_TILE], U32, align_bytes=64)
+        dconv_scales = operands.tile([P, PASSES, M_TILES, POSITIONS, M_TILE], U8, align_bytes=64)
         ec_codes = operands.tile([P, PASSES, GROUPS, L * ROW_COLS], U32, align_bytes=64)
         ec_scales = operands.tile([P, PASSES, GROUPS, L * ROW_COLS], U8, align_bytes=64)
         mask_pairs = {}
@@ -169,18 +164,25 @@ def tile_vrtconv_v_kernel(tc, Ec, W1, W2, W3, b1, b2, b3, conv2, grad_out, out):
 
         def dconv_of(g):
             g2_cols = grad_raw[g][:].rearrange("p o (t j h) -> p h j o t", t=PACK, j=K2, h=HEIGHTS)[:, 1]
-            for block in range(J_BLOCKS):
-                kernels = slice(block * J_BLOCK, (block + 1) * J_BLOCK)
-                block_cols = slice(block * BLOCK_COLS, (block + 1) * BLOCK_COLS)
-                quantise_dconv(
-                    nc,
-                    work,
-                    mask_pairs[g, block],
-                    g2_cols[:, kernels],
-                    nc.scalar.copy if block % 2 == 0 else nc.vector.tensor_copy,
-                    dconv_codes[:, g, :, block_cols],
-                    dconv_scales[:, g, :, block_cols],
+
+            def quantise(m, dconv):
+                nc.vector.quantize_mx(
+                    out=dconv_codes[:, g, m].rearrange("p q c -> p (q c)").bitcast(E5M2_X4),
+                    scales=dconv_scales[:, g, m].rearrange("p q c -> p (q c)"),
+                    in_=dconv.rearrange("p q w -> p (q w)"),
                 )
+
+            products = []
+            for m in range(M_TILES):
+                block, first = divmod(m * J_TILE, J_BLOCK)
+                tile_masks = mask_pairs[g, block][:, :, first : first + J_TILE].rearrange("p q j o t -> p q (j o t)")
+                copy_g2 = nc.vector.tensor_copy if m % 2 == 0 else nc.scalar.copy
+                products.append(
+                    multiply_dconv(nc, work, tile_masks, g2_cols[:, m * J_TILE : (m + 1) * J_TILE], copy_g2)
+                )
+                if m > 0:
+                    quantise(m - 1, products[m - 1][:])
+            quantise(M_TILES - 1, products[M_TILES - 1][:])
 
         def ec_of(group, g, vector_rows):
             quantise_ec(nc, stage, ec_raw[group, g], vector_rows, ec_codes[:, g, group, :], ec_scales[:, g, group, :])
@@ -191,13 +193,12 @@ def tile_vrtconv_v_kernel(tc, Ec, W1, W2, W3, b1, b2, b3, conv2, grad_out, out):
                 sums.append(psum.tile([M_TILE, N_TILE], F32, name="sums_%d" % m))
             for g in range(PASSES):
                 for m in range(M_TILES):
-                    m_rows = slice(m * M_TILE, (m + 1) * M_TILE)
                     for position in range(POSITIONS):
                         window = slice(position * ROW_COLS, position * ROW_COLS + N_TILE)
                         nc.tensor.matmul_mx(
                             out=sums[m][:],
-                            lhsT=dconv_codes[:, g, position, m_rows].bitcast(E5M2_X4),
-                            lhsT_scale=dconv_scales[:, g, position, m_rows],
+                            lhsT=dconv_codes[:, g, m, position].bitcast(E5M2_X4),
+                            lhsT_scale=dconv_scales[:, g, m, position],
                             rhs=ec_codes[:, g, group, window].bitcast(E4M3_X4),
                             rhs_scale=ec_scales[:, g, group, window],
                             start=(g == 0 and position == 0),

@@ -1,4 +1,5 @@
 import concourse.mybir as mybir
+from concourse.masks import make_identity
 
 F32 = mybir.dt.float32
 BF16 = mybir.dt.bfloat16
@@ -29,6 +30,10 @@ J_BLOCK = 8
 J_BLOCKS = K2 // J_BLOCK
 J_TILE = M_TILE // C
 LEAST = 2.0**-126
+HALVES = 2
+O_PARTS = 2
+O_PART = C // O_PARTS
+PSUM_BANKS = 8
 RUN = 4
 
 FLOPS = 2 * POSITIONS * (K2 * C) * (C * TAPS * D) * S
@@ -64,14 +69,23 @@ def make_masks(nc, work, conv_raw, mask_pair):
     )
 
 
-def multiply_dconv(nc, work, tile_masks, g2_cols, copy_g2):
-    g2 = work.tile([P, J_TILE, C, PACK], BF16)
-    copy_g2(out=g2[:], in_=g2_cols)
+def make_selectors(nc, pool):
+    identity = pool.tile([P, P // HALVES, HALVES], BF16)
+    make_identity(nc, identity[:].rearrange("p i h -> p (i h)"))
+    selectors = {}
+    for part in range(O_PARTS):
+        for half in range(HALVES):
+            selector = pool.tile([P, P // HALVES, HALVES], BF16, name="selector_%d_%d" % (part, half))
+            nc.vector.memset(selector[:], 0.0)
+            nc.vector.tensor_copy(out=selector[:, :, half], in_=identity[:, :, part])
+            selectors[part, half] = selector
+    return selectors
+
+
+def multiply_dconv(nc, work, tile_masks, g2):
     dconv = work.tile([P, POSITIONS, M_TILE * PACK], BF16, align_bytes=64)
     for position in range(POSITIONS):
-        nc.vector.tensor_tensor(
-            out=dconv[:, position], in0=tile_masks[:, position], in1=g2[:].rearrange("p j o t -> p (j o t)"), op=ALU.mult
-        )
+        nc.vector.tensor_tensor(out=dconv[:, position], in0=tile_masks[:, position], in1=g2, op=ALU.mult)
     return dconv
 
 
@@ -101,7 +115,7 @@ def tile_vrtconv_v_kernel(tc, Ec, W1, W2, W3, b1, b2, b3, conv2, grad_out, out):
     nc = tc.nc
 
     conv_rows = conv2.rearrange("q j (g p t) o -> g p (q j) (t o)", g=PASSES, p=P, t=PACK)
-    grad_rows = grad_out.rearrange("o (g p t) x n -> g p o (t x n)", g=PASSES, p=P, t=PACK)
+    grad_rows = grad_out.rearrange("(h o) (g i s) x n -> g h i o (s x n)", h=O_PARTS, g=PASSES, i=P // O_PARTS)
     ec_rows = Ec.rearrange("c (g p t) l d -> g p c (t l d)", g=PASSES, p=P, t=PACK)
     out_rows = out.rearrange("j o c a d -> (j o) (c a d)")
 
@@ -109,7 +123,8 @@ def tile_vrtconv_v_kernel(tc, Ec, W1, W2, W3, b1, b2, b3, conv2, grad_out, out):
         name="work", bufs=3
     ) as work, tc.tile_pool(name="stage", bufs=2 * L) as stage, tc.tile_pool(
         name="results", bufs=M_TILES
-    ) as results, tc.psum_pool(name="psum", bufs=2) as psum:
+    ) as results, tc.psum_pool(name="psum", bufs=PSUM_BANKS) as psum:
+        selectors = make_selectors(nc, operands)
         conv_raw = {}
         grad_raw = {}
         ec_raw = {}
@@ -132,8 +147,9 @@ def tile_vrtconv_v_kernel(tc, Ec, W1, W2, W3, b1, b2, b3, conv2, grad_out, out):
                         )
 
         def load_grad(g):
-            grad_raw[g] = inputs.tile([P, C, PACK * HEIGHTS * K2], BF16, name="grad_raw_%d" % g)
-            nc.sync.dma_start(out=grad_raw[g][:], in_=grad_rows[g])
+            grad_raw[g] = inputs.tile([P, O_PART, HALVES * PACK * HEIGHTS * K2], BF16, name="grad_raw_%d" % g)
+            for part in range(O_PARTS):
+                nc.sync.dma_start(out=grad_raw[g][part:P:O_PARTS], in_=grad_rows[g, part])
 
         def load_ec(group, g):
             ec_raw[group, g] = inputs.tile([P, C_GROUP, PACK * L * D], BF16, name="ec_raw_%d_%d" % (group, g))
@@ -141,9 +157,10 @@ def tile_vrtconv_v_kernel(tc, Ec, W1, W2, W3, b1, b2, b3, conv2, grad_out, out):
 
         load_conv(0)
         load_conv(1)
-        for g in range(PASSES):
-            load_grad(g)
-            load_ec(0, g)
+        load_grad(0)
+        load_ec(0, 0)
+        load_ec(0, 1)
+        load_grad(1)
         for group in range(1, GROUPS):
             for g in range(PASSES):
                 load_ec(group, g)
@@ -162,8 +179,32 @@ def tile_vrtconv_v_kernel(tc, Ec, W1, W2, W3, b1, b2, b3, conv2, grad_out, out):
                 for j in range(0, J_BLOCK, step):
                     make_masks(nc, work, conv_raw[g, block][:, :, j : j + step], mask_pair[:, :, j : j + step])
 
+        def g2_of(g):
+            g2_cols = grad_raw[g][:].rearrange("p o (s t j h) -> p h s j o t", s=HALVES, t=PACK, j=K2, h=HEIGHTS)[:, 1]
+            g2_blocks = []
+            for block in range(J_BLOCKS):
+                kernels = slice(block * J_BLOCK, (block + 1) * J_BLOCK)
+                copy_g2 = nc.vector.tensor_copy if block == 0 else nc.scalar.copy
+                runs = []
+                for half in range(HALVES):
+                    run = work.tile([P, J_BLOCK, O_PART * PACK], BF16, name="run_%d" % half)
+                    copy_g2(out=run[:].rearrange("p j (o t) -> p j o t", t=PACK), in_=g2_cols[:, half, kernels])
+                    runs.append(run)
+                g2 = psum.tile([P, J_BLOCK, O_PARTS, O_PART * PACK], BF16, name="bank")
+                for part in range(O_PARTS):
+                    for half in range(HALVES):
+                        nc.tensor.matmul(
+                            g2[:, :, part],
+                            lhsT=selectors[part, half][:].rearrange("p i h -> p (i h)"),
+                            rhs=runs[half][:],
+                            start=(half == 0),
+                            stop=(half == HALVES - 1),
+                        )
+                g2_blocks.append(g2)
+            return g2_blocks
+
         def dconv_of(g):
-            g2_cols = grad_raw[g][:].rearrange("p o (t j h) -> p h j o t", t=PACK, j=K2, h=HEIGHTS)[:, 1]
+            g2_blocks = g2_of(g)
 
             def quantise(m, dconv):
                 nc.vector.quantize_mx(
@@ -176,10 +217,8 @@ def tile_vrtconv_v_kernel(tc, Ec, W1, W2, W3, b1, b2, b3, conv2, grad_out, out):
             for m in range(M_TILES):
                 block, first = divmod(m * J_TILE, J_BLOCK)
                 tile_masks = mask_pairs[g, block][:, :, first : first + J_TILE].rearrange("p q j o t -> p q (j o t)")
-                copy_g2 = nc.vector.tensor_copy if m % 2 == 0 else nc.scalar.copy
-                products.append(
-                    multiply_dconv(nc, work, tile_masks, g2_cols[:, m * J_TILE : (m + 1) * J_TILE], copy_g2)
-                )
+                g2 = g2_blocks[block][:, first : first + J_TILE].rearrange("p j h w -> p (j h w)")
+                products.append(multiply_dconv(nc, work, tile_masks, g2))
                 if m > 0:
                     quantise(m - 1, products[m - 1][:])
             quantise(M_TILES - 1, products[M_TILES - 1][:])
@@ -190,7 +229,7 @@ def tile_vrtconv_v_kernel(tc, Ec, W1, W2, W3, b1, b2, b3, conv2, grad_out, out):
         def products_of(group):
             sums = []
             for m in range(M_TILES):
-                sums.append(psum.tile([M_TILE, N_TILE], F32, name="sums_%d" % m))
+                sums.append(psum.tile([M_TILE, N_TILE], F32, name="bank"))
             for g in range(PASSES):
                 for m in range(M_TILES):
                     for position in range(POSITIONS):

@@ -33,17 +33,15 @@ LEAST = 2.0**-126
 HALVES = 2
 O_PARTS = 2
 O_PART = C // O_PARTS
-PSUM_BANKS = 8
 RUN = 4
 
 FLOPS = 2 * POSITIONS * (K2 * C) * (C * TAPS * D) * S
 BYTES = 2 * C * S * L * D + 4 * POSITIONS * K2 * S * C + 2 * C * S * K2 + 4 * K2 * C * C * TAPS * D
 
 
-def make_masks(nc, work, conv_raw, mask_pair):
-    kernels = conv_raw.shape[2]
+def compare(nc, work, conv_raw):
     conv = conv_raw.rearrange("p q j w -> p q (j w)")
-    behind = work.tile([P, POSITIONS, kernels * PACK * C], BF16)
+    behind = work.tile([P, POSITIONS, J_TILE * PACK * C], BF16)
     for position in range(POSITIONS):
         nc.vector.scalar_tensor_tensor(
             out=behind[:, position],
@@ -53,15 +51,19 @@ def make_masks(nc, work, conv_raw, mask_pair):
             op0=ALU.max,
             op1=ALU.subtract,
         )
-    side = work.tile([P, POSITIONS * kernels, C, PACK], BF16)
+    side = work.tile([P, POSITIONS * J_TILE, C, PACK], BF16)
     nc.scalar.activation(
         out=side[:],
-        in_=behind[:].rearrange("p q (j t o) -> p (q j) o t", j=kernels, t=PACK, o=C),
+        in_=behind[:].rearrange("p q (j t o) -> p (q j) o t", j=J_TILE, t=PACK, o=C),
         func=ACT.Sign,
     )
+    return side
+
+
+def finish_masks(nc, side, tile_masks):
     nc.vector.tensor_scalar(
-        out=mask_pair,
-        in0=side[:].rearrange("p (q j) o t -> p q j o t", q=POSITIONS),
+        out=tile_masks,
+        in0=side.rearrange("p (q j) o t -> p q (j o t)", q=POSITIONS),
         scalar1=-0.5,
         scalar2=0.5,
         op0=ALU.mult,
@@ -82,6 +84,31 @@ def make_selectors(nc, pool):
     return selectors
 
 
+def fetch_g2(nc, work, g2_cols, on_vector):
+    runs = work.tile([P, HALVES, J_TILE, O_PART * PACK], BF16)
+    split = runs[:].rearrange("p h j (o t) -> p h j o t", t=PACK)
+    if on_vector:
+        nc.vector.tensor_copy(out=split, in_=g2_cols)
+    else:
+        for half in range(HALVES):
+            nc.scalar.copy(out=split[:, half], in_=g2_cols[:, half])
+    return runs
+
+
+def carry_g2(nc, psum, selectors, runs):
+    g2 = psum.tile([P, J_TILE, O_PARTS, O_PART * PACK], BF16, name="bank_a")
+    for part in range(O_PARTS):
+        for half in range(HALVES):
+            nc.tensor.matmul(
+                g2[:, :, part],
+                lhsT=selectors[part, half][:].rearrange("p i h -> p (i h)"),
+                rhs=runs[:, half],
+                start=(half == 0),
+                stop=(half == HALVES - 1),
+            )
+    return g2
+
+
 def multiply_dconv(nc, work, tile_masks, g2):
     dconv = work.tile([P, POSITIONS, M_TILE * PACK], BF16, align_bytes=64)
     for position in range(POSITIONS):
@@ -89,55 +116,42 @@ def multiply_dconv(nc, work, tile_masks, g2):
     return dconv
 
 
-def quantise_ec(nc, stage, ec_raw, vector_rows, codes, scales):
-    by_row = ec_raw[:].rearrange("p c (t l d) -> p l c d t", t=PACK, l=L, d=D)
-    grouped = []
-    for l in range(L):
-        ec_grouped = stage.tile([P, C_GROUP, D, PACK], BF16, align_bytes=64)
-        if l < vector_rows:
-            nc.vector.tensor_copy(
-                out=ec_grouped[:].rearrange("p c (e i) t -> p c e t i", i=RUN),
-                in_=by_row[:, l].rearrange("p c (e i) t -> p c e t i", i=RUN),
-            )
-        else:
-            nc.scalar.copy(out=ec_grouped[:], in_=by_row[:, l])
-        grouped.append(ec_grouped)
-    for l in range(L):
-        row_cols = slice(l * ROW_COLS, (l + 1) * ROW_COLS)
-        nc.vector.quantize_mx(
-            out=codes[:, row_cols].bitcast(E4M3_X4),
-            scales=scales[:, row_cols],
-            in_=grouped[l][:].rearrange("p c d t -> p (c d t)"),
+def regroup_row(nc, stage, ec_raw, l, on_vector):
+    by_row = ec_raw.rearrange("p c (t l d) -> p l c d t", t=PACK, l=L, d=D)[:, l]
+    grouped = stage.tile([P, C_GROUP, D, PACK], BF16, align_bytes=64)
+    if on_vector:
+        nc.vector.tensor_copy(
+            out=grouped[:].rearrange("p c (e i) t -> p c e t i", i=RUN),
+            in_=by_row.rearrange("p c (e i) t -> p c e t i", i=RUN),
         )
+    else:
+        nc.scalar.copy(out=grouped[:], in_=by_row)
+    return grouped
 
 
 def tile_vrtconv_v_kernel(tc, Ec, W1, W2, W3, b1, b2, b3, conv2, grad_out, out):
     nc = tc.nc
 
     conv_rows = conv2.rearrange("q j (g p t) o -> g p (q j) (t o)", g=PASSES, p=P, t=PACK)
-    grad_rows = grad_out.rearrange("(h o) (g i s) x n -> g h i o (s x n)", h=O_PARTS, g=PASSES, i=P // O_PARTS)
     ec_rows = Ec.rearrange("c (g p t) l d -> g p c (t l d)", g=PASSES, p=P, t=PACK)
+    grad_rows = grad_out.rearrange("(h o) (g i s) x n -> g h i o (s x n)", h=O_PARTS, g=PASSES, i=P // O_PARTS)
     out_rows = out.rearrange("j o c a d -> (j o) (c a d)")
 
     with tc.tile_pool(name="inputs", bufs=1) as inputs, tc.tile_pool(name="operands", bufs=1) as operands, tc.tile_pool(
-        name="work", bufs=3
-    ) as work, tc.tile_pool(name="stage", bufs=2 * L) as stage, tc.tile_pool(
-        name="results", bufs=M_TILES
-    ) as results, tc.psum_pool(name="psum", bufs=PSUM_BANKS) as psum:
-        selectors = make_selectors(nc, operands)
+        name="work", bufs=4
+    ) as work, tc.tile_pool(name="stage", bufs=3 * L) as stage, tc.tile_pool(
+        name="results", bufs=2 * M_TILES
+    ) as results, tc.psum_pool(name="psum", bufs=M_TILES) as psum, tc.manual_schedule():
         conv_raw = {}
         grad_raw = {}
         ec_raw = {}
-
-        def pieces_of(g, block):
-            return 2 if g == 0 and block == 0 else 1
 
         def load_conv(g):
             for block in range(J_BLOCKS):
                 conv_raw[g, block] = inputs.tile(
                     [P, POSITIONS, J_BLOCK, PACK * C], F32, name="conv_raw_%d_%d" % (g, block)
                 )
-                step = J_BLOCK // pieces_of(g, block)
+                step = J_TILE if (g, block) == (0, 0) else J_BLOCK
                 for j in range(0, J_BLOCK, step):
                     for position in range(POSITIONS):
                         first_j = position * K2 + block * J_BLOCK + j
@@ -165,97 +179,126 @@ def tile_vrtconv_v_kernel(tc, Ec, W1, W2, W3, b1, b2, b3, conv2, grad_out, out):
             for g in range(PASSES):
                 load_ec(group, g)
 
+        selectors = make_selectors(nc, operands)
+
         dconv_codes = operands.tile([P, PASSES, M_TILES, POSITIONS, M_TILE], U32, align_bytes=64)
         dconv_scales = operands.tile([P, PASSES, M_TILES, POSITIONS, M_TILE], U8, align_bytes=64)
         ec_codes = operands.tile([P, PASSES, GROUPS, L * ROW_COLS], U32, align_bytes=64)
         ec_scales = operands.tile([P, PASSES, GROUPS, L * ROW_COLS], U8, align_bytes=64)
-        mask_pairs = {}
+        masks_of = [
+            operands.tile([P, POSITIONS, M_TILES, M_TILE * PACK], BF16, name="masks_of_%d" % g) for g in range(PASSES)
+        ]
 
-        def masks_of(g):
-            for block in range(J_BLOCKS):
-                mask_pair = operands.tile([P, POSITIONS, J_BLOCK, C, PACK], BF16, name="mask_pair_%d_%d" % (g, block))
-                mask_pairs[g, block] = mask_pair
-                step = J_BLOCK // pieces_of(g, block)
-                for j in range(0, J_BLOCK, step):
-                    make_masks(nc, work, conv_raw[g, block][:, :, j : j + step], mask_pair[:, :, j : j + step])
+        def compare_tile(g, m):
+            block, first = divmod(m * J_TILE, J_BLOCK)
+            return compare(nc, work, conv_raw[g, block][:, :, first : first + J_TILE])
 
-        def g2_of(g):
+        def fetch_pass(g):
             g2_cols = grad_raw[g][:].rearrange("p o (s t j h) -> p h s j o t", s=HALVES, t=PACK, j=K2, h=HEIGHTS)[:, 1]
-            g2_blocks = []
-            for block in range(J_BLOCKS):
-                kernels = slice(block * J_BLOCK, (block + 1) * J_BLOCK)
-                copy_g2 = nc.vector.tensor_copy if block == 0 else nc.scalar.copy
-                runs = []
-                for half in range(HALVES):
-                    run = work.tile([P, J_BLOCK, O_PART * PACK], BF16, name="run_%d" % half)
-                    copy_g2(out=run[:].rearrange("p j (o t) -> p j o t", t=PACK), in_=g2_cols[:, half, kernels])
-                    runs.append(run)
-                g2 = psum.tile([P, J_BLOCK, O_PARTS, O_PART * PACK], BF16, name="bank")
-                for part in range(O_PARTS):
-                    for half in range(HALVES):
-                        nc.tensor.matmul(
-                            g2[:, :, part],
-                            lhsT=selectors[part, half][:].rearrange("p i h -> p (i h)"),
-                            rhs=runs[half][:],
-                            start=(half == 0),
-                            stop=(half == HALVES - 1),
-                        )
-                g2_blocks.append(g2)
-            return g2_blocks
+            carried = []
+            for m in range(M_TILES):
+                runs = fetch_g2(nc, work, g2_cols[:, :, m * J_TILE : (m + 1) * J_TILE], m % 2 == 0)
+                carried.append(carry_g2(nc, psum, selectors, runs[:]))
+            return carried
 
-        def dconv_of(g):
-            g2_blocks = g2_of(g)
+        def multiply_tile(g, m, carried):
+            return multiply_dconv(nc, work, masks_of[g][:, :, m], carried[m][:].rearrange("p j h w -> p (j h w)"))
 
-            def quantise(m, dconv):
-                nc.vector.quantize_mx(
-                    out=dconv_codes[:, g, m].rearrange("p q c -> p (q c)").bitcast(E5M2_X4),
-                    scales=dconv_scales[:, g, m].rearrange("p q c -> p (q c)"),
-                    in_=dconv.rearrange("p q w -> p (q w)"),
+        def quantise_tile(g, m, dconv):
+            nc.vector.quantize_mx(
+                out=dconv_codes[:, g, m].rearrange("p q c -> p (q c)").bitcast(E5M2_X4),
+                scales=dconv_scales[:, g, m].rearrange("p q c -> p (q c)"),
+                in_=dconv[:].rearrange("p q w -> p (q w)"),
+            )
+
+        def regroup(group, g, vector_rows):
+            return [regroup_row(nc, stage, ec_raw[group, g][:], l, l < vector_rows) for l in range(L)]
+
+        def quantise_row(group, g, l, grouped):
+            row_cols = slice(l * ROW_COLS, (l + 1) * ROW_COLS)
+            nc.vector.quantize_mx(
+                out=ec_codes[:, g, group, row_cols].bitcast(E4M3_X4),
+                scales=ec_scales[:, g, group, row_cols],
+                in_=grouped[l][:].rearrange("p c d t -> p (c d t)"),
+            )
+
+        def open_sums(group):
+            bank = "bank_b" if group % 2 == 0 else "bank_a"
+            return [psum.tile([M_TILE, N_TILE], F32, name=bank) for m in range(M_TILES)]
+
+        def products(group, g, sums, by_position):
+            if by_position:
+                order = [(m, position) for position in range(POSITIONS) for m in range(M_TILES)]
+            else:
+                order = [(m, position) for m in range(M_TILES) for position in range(POSITIONS)]
+            for m, position in order:
+                window = slice(position * ROW_COLS, position * ROW_COLS + N_TILE)
+                nc.tensor.matmul_mx(
+                    out=sums[m][:],
+                    lhsT=dconv_codes[:, g, m, position].bitcast(E5M2_X4),
+                    lhsT_scale=dconv_scales[:, g, m, position],
+                    rhs=ec_codes[:, g, group, window].bitcast(E4M3_X4),
+                    rhs_scale=ec_scales[:, g, group, window],
+                    start=(g == 0 and position == 0),
+                    stop=(g == PASSES - 1 and position == POSITIONS - 1),
                 )
 
-            products = []
-            for m in range(M_TILES):
-                block, first = divmod(m * J_TILE, J_BLOCK)
-                tile_masks = mask_pairs[g, block][:, :, first : first + J_TILE].rearrange("p q j o t -> p q (j o t)")
-                g2 = g2_blocks[block][:, first : first + J_TILE].rearrange("p j h w -> p (j h w)")
-                products.append(multiply_dconv(nc, work, tile_masks, g2))
-                if m > 0:
-                    quantise(m - 1, products[m - 1][:])
-            quantise(M_TILES - 1, products[M_TILES - 1][:])
+        def store(group, m, sums, copy_out):
+            result = results.tile([M_TILE, C_GROUP, TAPS, D], F32)
+            copy_out(out=result[:], in_=sums[m][:].rearrange("p (a c d) -> p c a d", a=TAPS, c=C_GROUP, d=D))
+            nc.sync.dma_start(
+                out=out_rows[m * M_TILE : (m + 1) * M_TILE, group * N_TILE : (group + 1) * N_TILE],
+                in_=result[:].rearrange("p c a d -> p (c a d)"),
+            )
 
-        def ec_of(group, g, vector_rows):
-            quantise_ec(nc, stage, ec_raw[group, g], vector_rows, ec_codes[:, g, group, :], ec_scales[:, g, group, :])
+        tiles = [(g, m) for g in range(PASSES) for m in range(M_TILES)]
+        side = compare_tile(*tiles[0])
+        for index, (g, m) in enumerate(tiles):
+            following = compare_tile(*tiles[index + 1]) if index + 1 < len(tiles) else None
+            finish_masks(nc, side[:], masks_of[g][:, :, m])
+            side = following
 
-        def products_of(group):
-            sums = []
-            for m in range(M_TILES):
-                sums.append(psum.tile([M_TILE, N_TILE], F32, name="bank"))
-            for g in range(PASSES):
-                for m in range(M_TILES):
-                    for position in range(POSITIONS):
-                        window = slice(position * ROW_COLS, position * ROW_COLS + N_TILE)
-                        nc.tensor.matmul_mx(
-                            out=sums[m][:],
-                            lhsT=dconv_codes[:, g, m, position].bitcast(E5M2_X4),
-                            lhsT_scale=dconv_scales[:, g, m, position],
-                            rhs=ec_codes[:, g, group, window].bitcast(E4M3_X4),
-                            rhs_scale=ec_scales[:, g, group, window],
-                            start=(g == 0 and position == 0),
-                            stop=(g == PASSES - 1 and position == POSITIONS - 1),
-                        )
-            for m in range(M_TILES):
-                result = results.tile([M_TILE, C_GROUP, TAPS, D], F32)
-                nc.scalar.copy(out=result[:], in_=sums[m][:].rearrange("p (a c d) -> p c a d", a=TAPS, c=C_GROUP, d=D))
-                nc.sync.dma_start(
-                    out=out_rows[m * M_TILE : (m + 1) * M_TILE, group * N_TILE : (group + 1) * N_TILE],
-                    in_=result[:].rearrange("p c a d -> p (c a d)"),
-                )
+        carried = fetch_pass(0)
+        grouped = regroup(0, 0, 0)
+        dconv = [multiply_tile(0, 0, carried)]
+        for m in range(1, M_TILES):
+            dconv.append(multiply_tile(0, m, carried))
+            quantise_tile(0, m - 1, dconv[m - 1])
+        quantise_row(0, 0, 0, grouped)
+        quantise_tile(0, M_TILES - 1, dconv[M_TILES - 1])
+        for l in range(1, L):
+            quantise_row(0, 0, l, grouped)
+        sums = {0: open_sums(0)}
+        products(0, 0, sums[0], False)
 
-        for g in range(PASSES):
-            masks_of(g)
-        for g in range(PASSES):
-            dconv_of(g)
-        for group in range(GROUPS):
-            for g in range(PASSES):
-                ec_of(group, g, 1 if group == 0 else L - 1)
-            products_of(group)
+        grouped = regroup(0, 1, 2)
+        for l in range(L - 1):
+            quantise_row(0, 1, l, grouped)
+        carried = fetch_pass(1)
+        quantise_row(0, 1, L - 1, grouped)
+        dconv = [multiply_tile(1, 0, carried)]
+        for m in range(1, M_TILES):
+            dconv.append(multiply_tile(1, m, carried))
+            quantise_tile(1, m - 1, dconv[m - 1])
+        grouped = regroup(1, 0, 1)
+        quantise_tile(1, M_TILES - 1, dconv[M_TILES - 1])
+        products(0, 1, sums[0], False)
+
+        waiting = [(0, m) for m in range(M_TILES)]
+        units = [(group, g) for group in range(1, GROUPS) for g in range(PASSES)]
+        for index, (group, g) in enumerate(units):
+            if index > 0:
+                grouped = regroup(group, g, 1 if group == 1 else 2)
+                for former, m in waiting[:2]:
+                    store(former, m, sums[former], nc.scalar.copy)
+                waiting = waiting[2:]
+            for l in range(L):
+                quantise_row(group, g, l, grouped)
+            if g == 0:
+                sums[group] = open_sums(group)
+            products(group, g, sums[group], index == len(units) - 1)
+            if g == PASSES - 1:
+                waiting += [(group, m) for m in range(M_TILES)]
+        for former, m in waiting:
+            on_vector = former == GROUPS - 1 and m % 2 == 1
+            store(former, m, sums[former], nc.vector.tensor_copy if on_vector else nc.scalar.copy)

@@ -26,13 +26,12 @@ C_GROUP = 8
 GROUPS = C // C_GROUP
 ROW_COLS = C_GROUP * D
 N_TILE = TAPS * ROW_COLS
-J_BLOCK = 8
-J_BLOCKS = K2 // J_BLOCK
 J_TILE = M_TILE // C
 LEAST = 2.0**-126
 HALVES = 2
 O_PARTS = 2
 O_PART = C // O_PARTS
+JOINED = 2
 RUN = 4
 
 FLOPS = 2 * POSITIONS * (K2 * C) * (C * TAPS * D) * S
@@ -140,25 +139,20 @@ def tile_vrtconv_v_kernel(tc, Ec, W1, W2, W3, b1, b2, b3, conv2, grad_out, out):
     with tc.tile_pool(name="inputs", bufs=1) as inputs, tc.tile_pool(name="operands", bufs=1) as operands, tc.tile_pool(
         name="work", bufs=4
     ) as work, tc.tile_pool(name="stage", bufs=3 * L) as stage, tc.tile_pool(
-        name="results", bufs=2 * M_TILES
+        name="results", bufs=M_TILES
     ) as results, tc.psum_pool(name="psum", bufs=M_TILES) as psum, tc.manual_schedule():
         conv_raw = {}
         grad_raw = {}
         ec_raw = {}
 
         def load_conv(g):
-            for block in range(J_BLOCKS):
-                conv_raw[g, block] = inputs.tile(
-                    [P, POSITIONS, J_BLOCK, PACK * C], F32, name="conv_raw_%d_%d" % (g, block)
-                )
-                step = J_TILE if (g, block) == (0, 0) else J_BLOCK
-                for j in range(0, J_BLOCK, step):
-                    for position in range(POSITIONS):
-                        first_j = position * K2 + block * J_BLOCK + j
-                        nc.sync.dma_start(
-                            out=conv_raw[g, block][:, position, j : j + step],
-                            in_=conv_rows[g][:, first_j : first_j + step, :],
-                        )
+            conv_raw[g] = inputs.tile([P, POSITIONS, K2, PACK * C], F32, name="conv_raw_%d" % g)
+            for first, last in ((0, 4), (4, 8), (8, 16)) if g == 0 else ((0, 8), (8, 16)):
+                for position in range(POSITIONS):
+                    nc.sync.dma_start(
+                        out=conv_raw[g][:, position, first:last],
+                        in_=conv_rows[g][:, position * K2 + first : position * K2 + last, :],
+                    )
 
         def load_grad(g):
             grad_raw[g] = inputs.tile([P, O_PART, HALVES * PACK * HEIGHTS * K2], BF16, name="grad_raw_%d" % g)
@@ -190,8 +184,7 @@ def tile_vrtconv_v_kernel(tc, Ec, W1, W2, W3, b1, b2, b3, conv2, grad_out, out):
         ]
 
         def compare_tile(g, m):
-            block, first = divmod(m * J_TILE, J_BLOCK)
-            return compare(nc, work, conv_raw[g, block][:, :, first : first + J_TILE])
+            return compare(nc, work, conv_raw[g][:, :, m * J_TILE : (m + 1) * J_TILE])
 
         def fetch_pass(g):
             g2_cols = grad_raw[g][:].rearrange("p o (s t j h) -> p h s j o t", s=HALVES, t=PACK, j=K2, h=HEIGHTS)[:, 1]
@@ -243,13 +236,24 @@ def tile_vrtconv_v_kernel(tc, Ec, W1, W2, W3, b1, b2, b3, conv2, grad_out, out):
                     stop=(g == PASSES - 1 and position == POSITIONS - 1),
                 )
 
+        half_stored = {}
+
         def store(group, m, sums, copy_out):
-            result = results.tile([M_TILE, C_GROUP, TAPS, D], F32)
-            copy_out(out=result[:], in_=sums[m][:].rearrange("p (a c d) -> p c a d", a=TAPS, c=C_GROUP, d=D))
-            nc.sync.dma_start(
-                out=out_rows[m * M_TILE : (m + 1) * M_TILE, group * N_TILE : (group + 1) * N_TILE],
-                in_=result[:].rearrange("p c a d -> p (c a d)"),
-            )
+            if group >= JOINED:
+                tile = results.tile([M_TILE, 1, C_GROUP, TAPS, D], F32, name="single")
+            elif group == 0:
+                tile = results.tile([M_TILE, JOINED, C_GROUP, TAPS, D], F32, name="joined")
+                half_stored[m] = tile
+            else:
+                tile = half_stored[m]
+            part = group if group < JOINED else 0
+            copy_out(out=tile[:, part], in_=sums[m][:].rearrange("p (a c d) -> p c a d", a=TAPS, c=C_GROUP, d=D))
+            if group > 0:
+                first = 0 if group < JOINED else group
+                nc.sync.dma_start(
+                    out=out_rows[m * M_TILE : (m + 1) * M_TILE, first * N_TILE : (group + 1) * N_TILE],
+                    in_=tile[:].rearrange("p k c a d -> p (k c a d)"),
+                )
 
         tiles = [(g, m) for g in range(PASSES) for m in range(M_TILES)]
         side = compare_tile(*tiles[0])
@@ -288,7 +292,7 @@ def tile_vrtconv_v_kernel(tc, Ec, W1, W2, W3, b1, b2, b3, conv2, grad_out, out):
         units = [(group, g) for group in range(1, GROUPS) for g in range(PASSES)]
         for index, (group, g) in enumerate(units):
             if index > 0:
-                grouped = regroup(group, g, 1 if group == 1 else 2)
+                grouped = regroup(group, g, 2)
                 for former, m in waiting[:2]:
                     store(former, m, sums[former], nc.scalar.copy)
                 waiting = waiting[2:]

@@ -84,7 +84,7 @@ def make_selectors(nc, pool):
 
 
 def fetch_g2(nc, work, g2_cols, on_vector):
-    runs = work.tile([P, HALVES, J_TILE, O_PART * PACK], BF16)
+    runs = work.tile([P, HALVES, J_TILE, O_PART * PACK], BF16, bufs=M_TILES)
     split = runs[:].rearrange("p h j (o t) -> p h j o t", t=PACK)
     if on_vector:
         nc.vector.tensor_copy(out=split, in_=g2_cols)
@@ -137,7 +137,7 @@ def tile_vrtconv_v_kernel(tc, Ec, W1, W2, W3, b1, b2, b3, conv2, grad_out, out):
     out_rows = out.rearrange("j o c a d -> (j o) (c a d)")
 
     with tc.tile_pool(name="inputs", bufs=1) as inputs, tc.tile_pool(name="operands", bufs=1) as operands, tc.tile_pool(
-        name="work", bufs=4
+        name="work", bufs=3
     ) as work, tc.tile_pool(name="stage", bufs=3 * L) as stage, tc.tile_pool(
         name="results", bufs=M_TILES
     ) as results, tc.psum_pool(name="psum", bufs=M_TILES) as psum, tc.manual_schedule():
@@ -240,7 +240,7 @@ def tile_vrtconv_v_kernel(tc, Ec, W1, W2, W3, b1, b2, b3, conv2, grad_out, out):
 
         def store(group, m, sums, copy_out):
             if group >= JOINED:
-                tile = results.tile([M_TILE, 1, C_GROUP, TAPS, D], F32, name="single")
+                tile = results.tile([M_TILE, 1, C_GROUP, TAPS, D], F32, name="single", bufs=2 * M_TILES)
             elif group == 0:
                 tile = results.tile([M_TILE, JOINED, C_GROUP, TAPS, D], F32, name="joined")
                 half_stored[m] = tile

@@ -110,8 +110,8 @@ def carry_g2(nc, psum, selectors, runs):
 
 def multiply_dconv(nc, work, tile_masks, g2):
     dconv = work.tile([P, POSITIONS, M_TILE * PACK], BF16, align_bytes=64)
-    for position in range(POSITIONS):
-        nc.vector.tensor_tensor(out=dconv[:, position], in0=tile_masks[:, position], in1=g2, op=ALU.mult)
+    both = g2.unsqueeze(1).to_broadcast([P, POSITIONS, M_TILE * PACK])
+    nc.vector.tensor_tensor(out=dconv[:], in0=tile_masks, in1=both, op=ALU.mult)
     return dconv
 
 
@@ -219,22 +219,19 @@ def tile_vrtconv_v_kernel(tc, Ec, W1, W2, W3, b1, b2, b3, conv2, grad_out, out):
             bank = "bank_b" if group % 2 == 0 else "bank_a"
             return [psum.tile([M_TILE, N_TILE], F32, name=bank) for m in range(M_TILES)]
 
-        def products(group, g, sums, by_position):
-            if by_position:
-                order = [(m, position) for position in range(POSITIONS) for m in range(M_TILES)]
-            else:
-                order = [(m, position) for m in range(M_TILES) for position in range(POSITIONS)]
-            for m, position in order:
-                window = slice(position * ROW_COLS, position * ROW_COLS + N_TILE)
-                nc.tensor.matmul_mx(
-                    out=sums[m][:],
-                    lhsT=dconv_codes[:, g, m, position].bitcast(E5M2_X4),
-                    lhsT_scale=dconv_scales[:, g, m, position],
-                    rhs=ec_codes[:, g, group, window].bitcast(E4M3_X4),
-                    rhs_scale=ec_scales[:, g, group, window],
-                    start=(g == 0 and position == 0),
-                    stop=(g == PASSES - 1 and position == POSITIONS - 1),
-                )
+        def products(group, g, sums):
+            for m in range(M_TILES):
+                for position in range(POSITIONS):
+                    window = slice(position * ROW_COLS, position * ROW_COLS + N_TILE)
+                    nc.tensor.matmul_mx(
+                        out=sums[m][:],
+                        lhsT=dconv_codes[:, g, m, position].bitcast(E5M2_X4),
+                        lhsT_scale=dconv_scales[:, g, m, position],
+                        rhs=ec_codes[:, g, group, window].bitcast(E4M3_X4),
+                        rhs_scale=ec_scales[:, g, group, window],
+                        start=(g == 0 and position == 0),
+                        stop=(g == PASSES - 1 and position == POSITIONS - 1),
+                    )
 
         half_stored = {}
 
@@ -273,7 +270,7 @@ def tile_vrtconv_v_kernel(tc, Ec, W1, W2, W3, b1, b2, b3, conv2, grad_out, out):
         for l in range(1, L):
             quantise_row(0, 0, l, grouped)
         sums = {0: open_sums(0)}
-        products(0, 0, sums[0], False)
+        products(0, 0, sums[0])
 
         grouped = regroup(0, 1, 2)
         for l in range(L - 1):
@@ -286,7 +283,7 @@ def tile_vrtconv_v_kernel(tc, Ec, W1, W2, W3, b1, b2, b3, conv2, grad_out, out):
             quantise_tile(1, m - 1, dconv[m - 1])
         grouped = regroup(1, 0, 1)
         quantise_tile(1, M_TILES - 1, dconv[M_TILES - 1])
-        products(0, 1, sums[0], False)
+        products(0, 1, sums[0])
 
         waiting = [(0, m) for m in range(M_TILES)]
         units = [(group, g) for group in range(1, GROUPS) for g in range(PASSES)]
@@ -300,7 +297,7 @@ def tile_vrtconv_v_kernel(tc, Ec, W1, W2, W3, b1, b2, b3, conv2, grad_out, out):
                 quantise_row(group, g, l, grouped)
             if g == 0:
                 sums[group] = open_sums(group)
-            products(group, g, sums[group], index == len(units) - 1)
+            products(group, g, sums[group])
             if g == PASSES - 1:
                 waiting += [(group, m) for m in range(M_TILES)]
         for former, m in waiting:

import concourse.mybir as mybir
from concourse.masks import make_identity

F32 = mybir.dt.float32
BF16 = mybir.dt.bfloat16
U32 = mybir.dt.uint32
U8 = mybir.dt.uint8
E4M3_X4 = mybir.dt.float8_e4m3fn_x4
E5M2_X4 = mybir.dt.float8_e5m2_x4
ALU = mybir.AluOpType
ACT = mybir.ActivationFunctionType

C, S, L, D = 32, 1024, 3, 32
HEIGHTS = 3
K2 = 16
POSITIONS = 2
TAPS = 2

P = 128
PACK = 4
PASSES = S // (P * PACK)

M_TILE = P
M_TILES = K2 * C // M_TILE
C_GROUP = 8
GROUPS = C // C_GROUP
ROW_COLS = C_GROUP * D
N_TILE = TAPS * ROW_COLS
J_TILE = M_TILE // C
LEAST = 2.0**-126
HALVES = 2
O_PARTS = 2
O_PART = C // O_PARTS
JOINED = 2
RUN = 4

FLOPS = 2 * POSITIONS * (K2 * C) * (C * TAPS * D) * S
BYTES = 2 * C * S * L * D + 4 * POSITIONS * K2 * S * C + 2 * C * S * K2 + 4 * K2 * C * C * TAPS * D


def compare(nc, work, conv_raw):
    conv = conv_raw.rearrange("p q j w -> p q (j w)")
    behind = work.tile([P, POSITIONS, J_TILE * PACK * C], BF16)
    for position in range(POSITIONS):
        nc.vector.scalar_tensor_tensor(
            out=behind[:, position],
            in0=conv[:, 1 - position],
            scalar=LEAST,
            in1=conv[:, position],
            op0=ALU.max,
            op1=ALU.subtract,
        )
    side = work.tile([P, POSITIONS * J_TILE, C, PACK], BF16)
    nc.scalar.activation(
        out=side[:],
        in_=behind[:].rearrange("p q (j t o) -> p (q j) o t", j=J_TILE, t=PACK, o=C),
        func=ACT.Sign,
    )
    return side


def finish_masks(nc, side, tile_masks):
    nc.vector.tensor_scalar(
        out=tile_masks,
        in0=side.rearrange("p (q j) o t -> p q (j o t)", q=POSITIONS),
        scalar1=-0.5,
        scalar2=0.5,
        op0=ALU.mult,
        op1=ALU.add,
    )


def make_selectors(nc, pool):
    identity = pool.tile([P, P // HALVES, HALVES], BF16)
    make_identity(nc, identity[:].rearrange("p i h -> p (i h)"))
    selectors = {}
    for part in range(O_PARTS):
        for half in range(HALVES):
            selector = pool.tile([P, P // HALVES, HALVES], BF16, name="selector_%d_%d" % (part, half))
            nc.vector.memset(selector[:], 0.0)
            nc.vector.tensor_copy(out=selector[:, :, half], in_=identity[:, :, part])
            selectors[part, half] = selector
    return selectors


def fetch_g2(nc, work, g2_cols, on_vector):
    runs = work.tile([P, HALVES, J_TILE, O_PART * PACK], BF16, bufs=M_TILES)
    split = runs[:].rearrange("p h j (o t) -> p h j o t", t=PACK)
    if on_vector:
        nc.vector.tensor_copy(out=split, in_=g2_cols)
    else:
        for half in range(HALVES):
            nc.scalar.copy(out=split[:, half], in_=g2_cols[:, half])
    return runs


def carry_g2(nc, psum, selectors, runs):
    g2 = psum.tile([P, J_TILE, O_PARTS, O_PART * PACK], BF16, name="bank_a")
    for part in range(O_PARTS):
        for half in range(HALVES):
            nc.tensor.matmul(
                g2[:, :, part],
                lhsT=selectors[part, half][:].rearrange("p i h -> p (i h)"),
                rhs=runs[:, half],
                start=(half == 0),
                stop=(half == HALVES - 1),
            )
    return g2


def multiply_dconv(nc, work, tile_masks, g2):
    dconv = work.tile([P, POSITIONS, M_TILE * PACK], BF16, align_bytes=64)
    both = g2.unsqueeze(1).to_broadcast([P, POSITIONS, M_TILE * PACK])
    nc.vector.tensor_tensor(out=dconv[:], in0=tile_masks, in1=both, op=ALU.mult)
    return dconv


def regroup_row(nc, stage, ec_raw, l, on_vector):
    by_row = ec_raw.rearrange("p c (t l d) -> p l c d t", t=PACK, l=L, d=D)[:, l]
    grouped = stage.tile([P, C_GROUP, D, PACK], BF16, align_bytes=64)
    if on_vector:
        nc.vector.tensor_copy(
            out=grouped[:].rearrange("p c (e i) t -> p c e t i", i=RUN),
            in_=by_row.rearrange("p c (e i) t -> p c e t i", i=RUN),
        )
    else:
        nc.scalar.copy(out=grouped[:], in_=by_row)
    return grouped


def tile_vrtconv_v_kernel(tc, Ec, W1, W2, W3, b1, b2, b3, conv2, grad_out, out):
    nc = tc.nc

    conv_rows = conv2.rearrange("q j (g p t) o -> g p (q j) (t o)", g=PASSES, p=P, t=PACK)
    ec_rows = Ec.rearrange("c (g p t) l d -> g p c (t l d)", g=PASSES, p=P, t=PACK)
    grad_rows = grad_out.rearrange("(h o) (g i s) x n -> g h i o (s x n)", h=O_PARTS, g=PASSES, i=P // O_PARTS)
    out_rows = out.rearrange("j o c a d -> (j o) (c a d)")

    with tc.tile_pool(name="inputs", bufs=1) as inputs, tc.tile_pool(name="operands", bufs=1) as operands, tc.tile_pool(
        name="work", bufs=3
    ) as work, tc.tile_pool(name="stage", bufs=3 * L) as stage, tc.tile_pool(
        name="results", bufs=M_TILES
    ) as results, tc.psum_pool(name="psum", bufs=M_TILES) as psum, tc.manual_schedule():
        conv_raw = {}
        grad_raw = {}
        ec_raw = {}

        def load_conv(g):
            conv_raw[g] = inputs.tile([P, POSITIONS, K2, PACK * C], F32, name="conv_raw_%d" % g)
            for first, last in ((0, 4), (4, 8), (8, 16)) if g == 0 else ((0, 8), (8, 16)):
                for position in range(POSITIONS):
                    nc.sync.dma_start(
                        out=conv_raw[g][:, position, first:last],
                        in_=conv_rows[g][:, position * K2 + first : position * K2 + last, :],
                    )

        def load_grad(g):
            grad_raw[g] = inputs.tile([P, O_PART, HALVES * PACK * HEIGHTS * K2], BF16, name="grad_raw_%d" % g)
            for part in range(O_PARTS):
                nc.sync.dma_start(out=grad_raw[g][part:P:O_PARTS], in_=grad_rows[g, part])

        def load_ec(group, g):
            ec_raw[group, g] = inputs.tile([P, C_GROUP, PACK * L * D], BF16, name="ec_raw_%d_%d" % (group, g))
            nc.sync.dma_start(out=ec_raw[group, g][:], in_=ec_rows[g][:, group * C_GROUP : (group + 1) * C_GROUP, :])

        load_conv(0)
        load_conv(1)
        load_grad(0)
        load_ec(0, 0)
        load_ec(0, 1)
        load_grad(1)
        for group in range(1, GROUPS):
            for g in range(PASSES):
                load_ec(group, g)

        selectors = make_selectors(nc, operands)

        dconv_codes = operands.tile([P, PASSES, M_TILES, POSITIONS, M_TILE], U32, align_bytes=64)
        dconv_scales = operands.tile([P, PASSES, M_TILES, POSITIONS, M_TILE], U8, align_bytes=64)
        ec_codes = operands.tile([P, PASSES, GROUPS, L * ROW_COLS], U32, align_bytes=64)
        ec_scales = operands.tile([P, PASSES, GROUPS, L * ROW_COLS], U8, align_bytes=64)
        masks_of = [
            operands.tile([P, POSITIONS, M_TILES, M_TILE * PACK], BF16, name="masks_of_%d" % g) for g in range(PASSES)
        ]

        def compare_tile(g, m):
            return compare(nc, work, conv_raw[g][:, :, m * J_TILE : (m + 1) * J_TILE])

        def fetch_pass(g):
            g2_cols = grad_raw[g][:].rearrange("p o (s t j h) -> p h s j o t", s=HALVES, t=PACK, j=K2, h=HEIGHTS)[:, 1]
            carried = []
            for m in range(M_TILES):
                runs = fetch_g2(nc, work, g2_cols[:, :, m * J_TILE : (m + 1) * J_TILE], m % 2 == 0)
                carried.append(carry_g2(nc, psum, selectors, runs[:]))
            return carried

        def multiply_tile(g, m, carried):
            return multiply_dconv(nc, work, masks_of[g][:, :, m], carried[m][:].rearrange("p j h w -> p (j h w)"))

        def quantise_tile(g, m, dconv):
            nc.vector.quantize_mx(
                out=dconv_codes[:, g, m].rearrange("p q c -> p (q c)").bitcast(E5M2_X4),
                scales=dconv_scales[:, g, m].rearrange("p q c -> p (q c)"),
                in_=dconv[:].rearrange("p q w -> p (q w)"),
            )

        def regroup(group, g, vector_rows):
            return [regroup_row(nc, stage, ec_raw[group, g][:], l, l < vector_rows) for l in range(L)]

        def quantise_row(group, g, l, grouped):
            row_cols = slice(l * ROW_COLS, (l + 1) * ROW_COLS)
            nc.vector.quantize_mx(
                out=ec_codes[:, g, group, row_cols].bitcast(E4M3_X4),
                scales=ec_scales[:, g, group, row_cols],
                in_=grouped[l][:].rearrange("p c d t -> p (c d t)"),
            )

        def open_sums(group):
            bank = "bank_b" if group % 2 == 0 else "bank_a"
            return [psum.tile([M_TILE, N_TILE], F32, name=bank) for m in range(M_TILES)]

        def products(group, g, sums):
            for m in range(M_TILES):
                for position in range(POSITIONS):
                    window = slice(position * ROW_COLS, position * ROW_COLS + N_TILE)
                    nc.tensor.matmul_mx(
                        out=sums[m][:],
                        lhsT=dconv_codes[:, g, m, position].bitcast(E5M2_X4),
                        lhsT_scale=dconv_scales[:, g, m, position],
                        rhs=ec_codes[:, g, group, window].bitcast(E4M3_X4),
                        rhs_scale=ec_scales[:, g, group, window],
                        start=(g == 0 and position == 0),
                        stop=(g == PASSES - 1 and position == POSITIONS - 1),
                    )

        half_stored = {}

        def store(group, m, sums, copy_out):
            if group >= JOINED:
                tile = results.tile([M_TILE, 1, C_GROUP, TAPS, D], F32, name="single", bufs=2 * M_TILES)
            elif group == 0:
                tile = results.tile([M_TILE, JOINED, C_GROUP, TAPS, D], F32, name="joined")
                half_stored[m] = tile
            else:
                tile = half_stored[m]
            part = group if group < JOINED else 0
            copy_out(out=tile[:, part], in_=sums[m][:].rearrange("p (a c d) -> p c a d", a=TAPS, c=C_GROUP, d=D))
            if group > 0:
                first = 0 if group < JOINED else group
                nc.sync.dma_start(
                    out=out_rows[m * M_TILE : (m + 1) * M_TILE, first * N_TILE : (group + 1) * N_TILE],
                    in_=tile[:].rearrange("p k c a d -> p (k c a d)"),
                )

        tiles = [(g, m) for g in range(PASSES) for m in range(M_TILES)]
        side = compare_tile(*tiles[0])
        for index, (g, m) in enumerate(tiles):
            following = compare_tile(*tiles[index + 1]) if index + 1 < len(tiles) else None
            finish_masks(nc, side[:], masks_of[g][:, :, m])
            side = following

        carried = fetch_pass(0)
        grouped = regroup(0, 0, 0)
        dconv = [multiply_tile(0, 0, carried)]
        for m in range(1, M_TILES):
            dconv.append(multiply_tile(0, m, carried))
            quantise_tile(0, m - 1, dconv[m - 1])
        quantise_row(0, 0, 0, grouped)
        quantise_tile(0, M_TILES - 1, dconv[M_TILES - 1])
        for l in range(1, L):
            quantise_row(0, 0, l, grouped)
        sums = {0: open_sums(0)}
        products(0, 0, sums[0])

        grouped = regroup(0, 1, 2)
        for l in range(L - 1):
            quantise_row(0, 1, l, grouped)
        carried = fetch_pass(1)
        quantise_row(0, 1, L - 1, grouped)
        dconv = [multiply_tile(1, 0, carried)]
        for m in range(1, M_TILES):
            dconv.append(multiply_tile(1, m, carried))
            quantise_tile(1, m - 1, dconv[m - 1])
        grouped = regroup(1, 0, 1)
        quantise_tile(1, M_TILES - 1, dconv[M_TILES - 1])
        products(0, 1, sums[0])

        waiting = [(0, m) for m in range(M_TILES)]
        units = [(group, g) for group in range(1, GROUPS) for g in range(PASSES)]
        for index, (group, g) in enumerate(units):
            if index > 0:
                grouped = regroup(group, g, 2)
                for former, m in waiting[:2]:
                    store(former, m, sums[former], nc.scalar.copy)
                waiting = waiting[2:]
            for l in range(L):
                quantise_row(group, g, l, grouped)
            if g == 0:
                sums[group] = open_sums(group)
            products(group, g, sums[group])
            if g == PASSES - 1:
                waiting += [(group, m) for m in range(M_TILES)]
        for former, m in waiting:
            on_vector = former == GROUPS - 1 and m % 2 == 1
            store(former, m, sums[former], nc.vector.tensor_copy if on_vector else nc.scalar.copy)
